import numpy as np
import ml_dtypes


def mxq(x, axis, fmt="e4m3"):
    dtype, down = {"e4m3": (ml_dtypes.float8_e4m3fn, 7), "e5m2": (ml_dtypes.float8_e5m2, 14)}[fmt]
    v = np.moveaxis(np.asarray(x, np.float32).astype(ml_dtypes.bfloat16).astype(np.float64), axis, -1)
    blocks = v.reshape(v.shape[:-1] + (-1, 32))
    amax = np.abs(blocks).max(-1, keepdims=True)
    byte = np.maximum(np.where(amax > 0, np.frexp(amax)[1] - 1 + 127, 0) - down, 1)
    scale = np.exp2(byte - 127.0)
    codes = (blocks / scale).astype(np.float32).astype(dtype).astype(np.float64)
    return np.moveaxis((codes * scale).reshape(v.shape), -1, axis)


WIDE = False


def mx_kscale(k):
    if not WIDE:
        return np.ones(k)
    levels = np.array([10, -10, 5, -5, 0])
    if k % 512:
        return np.exp2(np.random.permutation(np.resize(levels, k // 32))).repeat(32)
    a = np.empty((k // 512, 16))
    for p in range(k // 512):
        a[p, :8] = np.random.permutation(np.resize(levels, 8))
        for g in range(8):
            far = levels[np.abs(levels - a[p, g]) >= 10]
            a[p, g + 8] = far[np.random.randint(len(far))]
    return np.exp2(a.ravel()).repeat(32)


BF16 = ml_dtypes.bfloat16


def bf(x):
    return np.asarray(x, np.float32).astype(BF16)


def f64(x):
    return np.asarray(x).astype(np.float64)


S, D, H, HD, CQ, CKV, O = 1024, 2048, 16, 128, 96, 512, 2048
E = H * HD
ROPE_BASE = 10000.0


def rope(xh, cos, sin):
    half = xh.shape[-1] // 2
    x1, x2 = xh[..., :half], xh[..., half:]
    rot = np.concatenate([-x2, x1], axis=-1)
    return xh * cos[:, None, :] + rot * sin[:, None, :]


def setup_inputs():
    s, t = mx_kscale(D), mx_kscale(CKV)
    pos = np.arange(S, dtype=np.float64)[:, None]
    inv_freq = 1.0 / (ROPE_BASE ** (np.arange(0, HD, 2, dtype=np.float64) / HD))
    ang = pos * inv_freq[None, :]
    return {"x": bf(np.random.standard_normal((S, D)) * s[None, :]),
            "rope_cos": bf(np.concatenate([np.cos(ang), np.cos(ang)], axis=-1)),
            "rope_sin": bf(np.concatenate([np.sin(ang), np.sin(ang)], axis=-1)),
            "wkv_down": bf(np.random.standard_normal((CKV, D)) / np.sqrt(D) * t[:, None] / s[None, :]),
            "bkv_down": bf(np.random.standard_normal(CKV) * 0.3 * t),
            "wk_up": bf(np.random.standard_normal((E, CKV)) / np.sqrt(CKV) / t[None, :]),
            "bk_up": bf(np.random.standard_normal(E) * 0.3),
            "wv_up": bf(np.random.standard_normal((E, CKV)) / np.sqrt(CKV) / t[None, :]),
            "bv_up": bf(np.random.standard_normal(E) * 0.3)}


def reference(x, rope_cos, rope_sin, wkv_down, bkv_down, wk_up, bk_up, wv_up, bv_up):
    c_kv = (mxq(f64(x), 1, "e4m3") @ mxq(f64(wkv_down), 1, "e4m3").T) + f64(bkv_down)
    cq = mxq(c_kv, 1, "e4m3")
    k = ((cq @ mxq(f64(wk_up), 1, "e4m3").T) + f64(bk_up)).reshape(S, H, HD)
    v = ((cq @ mxq(f64(wv_up), 1, "e4m3").T) + f64(bv_up)).reshape(S, H, HD)
    return rope(k, f64(rope_cos), f64(rope_sin)), v

@@ -1,0 +1,305 @@
+from contextlib import ExitStack
+
+import concourse.mybir as mybir
+from concourse.masks import make_identity
+
+F32 = mybir.dt.float32
+BF16 = mybir.dt.bfloat16
+U32 = mybir.dt.uint32
+U8 = mybir.dt.uint8
+FP8X4 = mybir.dt.float8_e4m3fn_x4
+ADD = mybir.AluOpType.add
+SUBTRACT = mybir.AluOpType.subtract
+MULT = mybir.AluOpType.mult
+IDENTITY = mybir.ActivationFunctionType.Identity
+
+P = 128
+PACK = 4
+K_PASS = P * PACK
+WORDS = K_PASS // 2
+BANK = 512
+
+S, D, CKV, HEADS, HEAD_DIM = 1024, 2048, 512, 16, 128
+E = HEADS * HEAD_DIM
+HALF_DIM = HEAD_DIM // 2
+S_TILES = S // P
+S_HALVES = S // BANK
+TILES = BANK // P
+D_PASSES = D // K_PASS
+CHUNKS = E // BANK
+CHUNK_HEADS = BANK // HEAD_DIM
+
+FLOPS = 2 * S * D * CKV + 2 * 2 * S * CKV * E
+
+
+def quantise_rows(nc, banks, stage, identity, copies, raw_words, codes, scales):
+    row_tiles = raw_words.shape[1]
+    grouped = stage.tile([P, 4 * P, PACK], BF16, tag="grouped", align_bytes=64)
+    grouped_words = grouped[:].bitcast(F32)
+    for first in range(0, row_tiles, 2):
+        bank = banks.tile([P, 2, 2, P], F32, tag="turned", bufs=4)
+        for r in range(2):
+            for u in range(2):
+                nc.tensor.transpose(
+                    bank[:, r, u, :], raw_words[:, first + r, u:WORDS:2], identity[:]
+                )
+        copies[first // 2](
+            out=grouped_words[:, first * P : (first + 2) * P, :].rearrange(
+                "p (r row) u -> p r row u", r=2
+            ),
+            in_=bank[:].rearrange("p r u row -> p r row u"),
+        )
+    nc.vector.quantize_mx(
+        out=codes.bitcast(FP8X4),
+        scales=scales,
+        in_=grouped[:, : row_tiles * P, :].rearrange("p row t -> p (row t)"),
+    )
+
+
+def tile_selfattention_pa_kernel(
+    tc, x, rope_cos, rope_sin, wkv_down, bkv_down, wk_up, bk_up, wv_up, bv_up, out_0, out_1
+):
+    nc = tc.nc
+    with ExitStack() as pools:
+        keep = pools.enter_context(tc.tile_pool(name="keep", bufs=1))
+        stage = pools.enter_context(tc.tile_pool(name="stage", bufs=4))
+        results = pools.enter_context(tc.tile_pool(name="results", bufs=4))
+        banks = pools.enter_context(tc.psum_pool(name="banks", bufs=2))
+        pools.enter_context(tc.manual_schedule())
+
+        identity = keep.tile([P, P], F32)
+        make_identity(nc, identity[:])
+
+        wkv_raw = keep.tile([P, PACK, D], BF16)
+        wkv_rows = wkv_down.rearrange("(p t) d -> p t d", t=PACK)
+        for u in range(2):
+            nc.sync.dma_start(out=wkv_raw[:, 2 * u : 2 * u + 2, :], in_=wkv_rows[:, 2 * u : 2 * u + 2, :])
+        bkv_bf16 = keep.tile([P, PACK], BF16)
+        nc.sync.dma_start(out=bkv_bf16[:], in_=bkv_down.rearrange("(p t) -> p t", t=PACK))
+
+        x_raw = keep.tile([P, S_TILES, D], BF16)
+        x_rows = x.rearrange("(j p) d -> p j d", p=P)
+        wk_raw = keep.tile([P, HEADS, CKV], BF16)
+        wk_rows = wk_up.rearrange("(h p) c -> p h c", p=P)
+        wv_raw = keep.tile([P, HEADS, CKV], BF16)
+        wv_rows = wv_up.rearrange("(h p) c -> p h c", p=P)
+
+        def load_x_half(half):
+            for j in range(half * TILES, (half + 1) * TILES, 2):
+                nc.sync.dma_start(out=x_raw[:, j : j + 2, :], in_=x_rows[:, j : j + 2, :])
+
+        def load_up_weights(q):
+            heads = slice(q * CHUNK_HEADS, (q + 1) * CHUNK_HEADS)
+            nc.sync.dma_start(out=wk_raw[:, heads, :], in_=wk_rows[:, heads, :])
+            nc.sync.dma_start(out=wv_raw[:, heads, :], in_=wv_rows[:, heads, :])
+
+        load_x_half(0)
+        load_up_weights(0)
+        bk_bf16 = keep.tile([P, HEADS], BF16)
+        with nc.allow_non_contiguous_dma(reason="a 4 KiB bias, one element to a partition"):
+            nc.sync.dma_start(out=bk_bf16[:], in_=bk_up.rearrange("(h d) -> d h", d=HEAD_DIM))
+        tables = keep.tile([P, S_TILES, 2, HEAD_DIM], BF16)
+        sin_raw = keep.tile([P, S_TILES, HEAD_DIM], BF16)
+        nc.sync.dma_start(out=tables[:, :, 0, :], in_=rope_cos.rearrange("(j p) d -> p j d", p=P))
+        nc.sync.dma_start(out=sin_raw[:], in_=rope_sin.rearrange("(j p) d -> p j d", p=P))
+        nc.gpsimd.tensor_copy(out=tables[:, :, 1, :HALF_DIM], in_=sin_raw[:, :, HALF_DIM:])
+        nc.gpsimd.tensor_copy(out=tables[:, :, 1, HALF_DIM:], in_=sin_raw[:, :, :HALF_DIM])
+        bv_all = keep.tile([P, E], BF16)
+        nc.sync.dma_start(out=bv_all[:], in_=bv_up.partition_broadcast(P))
+        for q in range(1, CHUNKS):
+            load_up_weights(q)
+        load_x_half(1)
+
+        wkv_codes = keep.tile([P, D_PASSES, CKV], U32, align_bytes=64)
+        wkv_scales = keep.tile([P, D_PASSES, CKV], U8, align_bytes=64)
+        x_codes = keep.tile([P, D_PASSES, S], U32, align_bytes=64)
+        x_scales = keep.tile([P, D_PASSES, S], U8, align_bytes=64)
+        c_codes = keep.tile([P, S], U32, align_bytes=64)
+        c_scales = keep.tile([P, S], U8, align_bytes=64)
+        wk_codes = keep.tile([P, E], U32, align_bytes=64)
+        wk_scales = keep.tile([P, E], U8, align_bytes=64)
+        wv_codes = keep.tile([P, E], U32, align_bytes=64)
+        wv_scales = keep.tile([P, E], U8, align_bytes=64)
+
+        wkv_words = wkv_raw[:].bitcast(F32)
+        x_words = x_raw[:].bitcast(F32)
+        wk_words = wk_raw[:].bitcast(F32)
+        wv_words = wv_raw[:].bitcast(F32)
+
+        def quantise_wkv(g, copies):
+            quantise_rows(
+                nc, banks, stage, identity, copies,
+                wkv_words[:, :, g * WORDS : (g + 1) * WORDS], wkv_codes[:, g, :], wkv_scales[:, g, :],
+            )
+
+        def quantise_x(first_tile, tiles, g, copies):
+            cols = slice(first_tile * P, (first_tile + tiles) * P)
+            quantise_rows(
+                nc, banks, stage, identity, copies,
+                x_words[:, first_tile : first_tile + tiles, g * WORDS : (g + 1) * WORDS],
+                x_codes[:, g, cols], x_scales[:, g, cols],
+            )
+
+        def quantise_wk(q, copies):
+            cols = slice(q * BANK, (q + 1) * BANK)
+            quantise_rows(
+                nc, banks, stage, identity, copies,
+                wk_words[:, q * CHUNK_HEADS : (q + 1) * CHUNK_HEADS, :],
+                wk_codes[:, cols], wk_scales[:, cols],
+            )
+
+        def quantise_wv(q, copies):
+            cols = slice(q * BANK, (q + 1) * BANK)
+            quantise_rows(
+                nc, banks, stage, identity, copies,
+                wv_words[:, q * CHUNK_HEADS : (q + 1) * CHUNK_HEADS, :],
+                wv_codes[:, cols], wv_scales[:, cols],
+            )
+
+        bkv = keep.tile([P, PACK], F32)
+        bk = keep.tile([P, HEADS], F32)
+        c_rows = keep.tile([P, S_HALVES, PACK, BANK], BF16)
+
+        def compress(half, t):
+            pos = slice(half * BANK, (half + 1) * BANK)
+            rows = slice(t * P, (t + 1) * P)
+            c_bank = banks.tile([P, BANK], F32, tag="for_scalar")
+            for g in range(D_PASSES):
+                nc.tensor.matmul_mx(
+                    out=c_bank[:],
+                    lhsT=wkv_codes[:, g, rows].bitcast(FP8X4),
+                    lhsT_scale=wkv_scales[:, g, rows],
+                    rhs=x_codes[:, g, pos].bitcast(FP8X4),
+                    rhs_scale=x_scales[:, g, pos],
+                    start=(g == 0),
+                    stop=(g == D_PASSES - 1),
+                )
+            nc.scalar.activation(
+                out=c_rows[:, half, t, :], in_=c_bank[:], func=IDENTITY, bias=bkv[:, t : t + 1],
+                scale=1.0,
+            )
+
+        def quantise_c(half):
+            pos = slice(half * BANK, (half + 1) * BANK)
+            c_grouped = stage.tile([P, BANK, PACK], BF16, tag="grouped", align_bytes=64)
+            nc.vector.tensor_copy(out=c_grouped[:], in_=c_rows[:, half].rearrange("p t s -> p s t"))
+            nc.vector.quantize_mx(
+                out=c_codes[:, pos].bitcast(FP8X4),
+                scales=c_scales[:, pos],
+                in_=c_grouped[:].rearrange("p s t -> p (s t)"),
+            )
+
+        def project_key_head(half, h):
+            pos = slice(half * BANK, (half + 1) * BANK)
+            cols = slice(h * HEAD_DIM, (h + 1) * HEAD_DIM)
+            kT_bank = banks.tile([P, BANK], F32, tag="for_scalar")
+            nc.tensor.matmul_mx(
+                out=kT_bank[:],
+                lhsT=wk_codes[:, cols].bitcast(FP8X4),
+                lhsT_scale=wk_scales[:, cols],
+                rhs=c_codes[:, pos].bitcast(FP8X4),
+                rhs_scale=c_scales[:, pos],
+                start=True,
+                stop=True,
+            )
+            kT = stage.tile([P, BANK], F32, tag="kT")
+            nc.scalar.activation(
+                out=kT[:], in_=kT_bank[:], func=IDENTITY, bias=bk[:, h : h + 1], scale=1.0
+            )
+            return kT
+
+        def project_values(j, q, v_rows):
+            pos = slice(j * P, (j + 1) * P)
+            cols = slice(q * BANK, (q + 1) * BANK)
+            v_bank = banks.tile([P, BANK], F32, tag="for_vector")
+            nc.tensor.matmul_mx(
+                out=v_bank[:],
+                lhsT=c_codes[:, pos].bitcast(FP8X4),
+                lhsT_scale=c_scales[:, pos],
+                rhs=wv_codes[:, cols].bitcast(FP8X4),
+                rhs_scale=wv_scales[:, cols],
+                start=True,
+                stop=True,
+            )
+            nc.vector.tensor_tensor(out=v_rows, in0=v_bank[:], in1=bv_all[:, cols], op=ADD)
+
+        def rope_products(half, kT, products):
+            k_bank = banks.tile([P, TILES, HEAD_DIM], F32, tag="turned", bufs=4)
+            for jj in range(TILES):
+                nc.tensor.transpose(k_bank[:, jj, :], kT[:, jj * P : (jj + 1) * P], identity[:])
+            nc.vector.tensor_tensor(
+                out=products,
+                in0=k_bank[:].unsqueeze(1).to_broadcast([P, 2, TILES, HEAD_DIM]),
+                in1=tables[:, half * TILES : (half + 1) * TILES].rearrange("p j c d -> p c j d"),
+                op=MULT,
+            )
+
+        def rope_sums(products):
+            nc.gpsimd.tensor_tensor(
+                out=products[:, 0, :, :, :HALF_DIM],
+                in0=products[:, 0, :, :, :HALF_DIM],
+                in1=products[:, 1, :, :, HALF_DIM:],
+                op=SUBTRACT,
+            )
+            nc.gpsimd.tensor_tensor(
+                out=products[:, 0, :, :, HALF_DIM:],
+                in0=products[:, 0, :, :, HALF_DIM:],
+                in1=products[:, 1, :, :, :HALF_DIM],
+                op=ADD,
+            )
+
+        nc.vector.tensor_copy(out=bkv[:], in_=bkv_bf16[:])
+        scalar_only = (nc.scalar.copy, nc.scalar.copy)
+        shared = (nc.scalar.copy, nc.vector.tensor_copy)
+        for g in range(D_PASSES):
+            quantise_wkv(g, shared)
+        for first_tile in range(0, TILES, 2):
+            for g in range(D_PASSES):
+                quantise_x(first_tile, 2, g, scalar_only)
+        quantise_wv(0, shared)
+        quantise_wk(0, shared)
+        nc.vector.tensor_copy(out=bk[:], in_=bk_bf16[:])
+        for t in range(PACK):
+            compress(0, t)
+        quantise_c(0)
+
+        later = []
+        for q in range(1, CHUNKS):
+            later.append((quantise_wk, (q, scalar_only)))
+            later.append((quantise_wv, (q, scalar_only)))
+        for g in range(D_PASSES):
+            later.append((quantise_x, (TILES, TILES, g, scalar_only)))
+        for t in range(PACK):
+            later.append((compress, (1, t)))
+        later.append((quantise_c, (1,)))
+
+        steps = [(half, h) for half in range(S_HALVES) for h in range(HEADS)]
+        kT_next = project_key_head(*steps[0])
+        for step, (half, h) in enumerate(steps):
+            q, i = divmod(h, CHUNK_HEADS)
+            j = half * TILES + i
+            if h % 2 == 0:
+                products = results.tile([P, 2, TILES, 2, HEAD_DIM], F32, tag="products")
+                v_rows = results.tile([P, 2, BANK], F32, tag="v_rows")
+            kT = kT_next
+            if step + 1 < len(steps):
+                kT_next = project_key_head(*steps[step + 1])
+            project_values(j, q, v_rows[:, h % 2, :])
+            rope_products(half, kT, products[:, :, :, h % 2, :])
+            if step < len(later):
+                piece, arguments = later[step]
+                piece(*arguments)
+            if h % 2 == 1:
+                rope_sums(products)
+                nc.sync.dma_start(
+                    out=out_1[
+                        (j - 1) * P : (j + 1) * P, q * CHUNK_HEADS : (q + 1) * CHUNK_HEADS, :
+                    ].rearrange("(r p) h d -> p r (h d)", p=P),
+                    in_=v_rows[:],
+                )
+                nc.sync.dma_start(
+                    out=out_0[half * BANK : (half + 1) * BANK, h - 1 : h + 1, :].rearrange(
+                        "(j p) h d -> p j h d", p=P
+                    ),
+                    in_=products[:, 0],
+                )

@@ -23,37 +23,14 @@ S, D, CKV, HEADS, HEAD_DIM = 1024, 2048, 512, 16, 128
 E = HEADS * HEAD_DIM
 HALF_DIM = HEAD_DIM // 2
 S_TILES = S // P
-S_HALVES = S // BANK
 TILES = BANK // P
+PAIR = 2 * P
+PAIRS = S // PAIR
 D_PASSES = D // K_PASS
 CHUNKS = E // BANK
 CHUNK_HEADS = BANK // HEAD_DIM
 
 FLOPS = 2 * S * D * CKV + 2 * 2 * S * CKV * E
-
-
-def quantise_rows(nc, banks, stage, identity, copies, raw_words, codes, scales):
-    row_tiles = raw_words.shape[1]
-    grouped = stage.tile([P, 4 * P, PACK], BF16, tag="grouped", align_bytes=64)
-    grouped_words = grouped[:].bitcast(F32)
-    for first in range(0, row_tiles, 2):
-        bank = banks.tile([P, 2, 2, P], F32, tag="turned", bufs=4)
-        for r in range(2):
-            for u in range(2):
-                nc.tensor.transpose(
-                    bank[:, r, u, :], raw_words[:, first + r, u:WORDS:2], identity[:]
-                )
-        copies[first // 2](
-            out=grouped_words[:, first * P : (first + 2) * P, :].rearrange(
-                "p (r row) u -> p r row u", r=2
-            ),
-            in_=bank[:].rearrange("p r u row -> p r row u"),
-        )
-    nc.vector.quantize_mx(
-        out=codes.bitcast(FP8X4),
-        scales=scales,
-        in_=grouped[:, : row_tiles * P, :].rearrange("p row t -> p (row t)"),
-    )
 
 
 def tile_selfattention_pa_kernel(
@@ -62,38 +39,46 @@ def tile_selfattention_pa_kernel(
     nc = tc.nc
     with ExitStack() as pools:
         keep = pools.enter_context(tc.tile_pool(name="keep", bufs=1))
-        stage = pools.enter_context(tc.tile_pool(name="stage", bufs=4))
-        results = pools.enter_context(tc.tile_pool(name="results", bufs=4))
+        raw = pools.enter_context(tc.tile_pool(name="raw", bufs=16))
+        stage = pools.enter_context(tc.tile_pool(name="stage", bufs=3))
+        results = pools.enter_context(tc.tile_pool(name="results", bufs=3))
         banks = pools.enter_context(tc.psum_pool(name="banks", bufs=2))
         pools.enter_context(tc.manual_schedule())
 
         identity = keep.tile([P, P], F32)
         make_identity(nc, identity[:])
 
-        wkv_raw = keep.tile([P, PACK, D], BF16)
+        def load_piece(shape, source):
+            piece = raw.tile([P] + shape, BF16, tag="piece", name="piece")
+            nc.sync.dma_start(out=piece[:], in_=source)
+            return piece
+
         wkv_rows = wkv_down.rearrange("(p t) d -> p t d", t=PACK)
-        for u in range(2):
-            nc.sync.dma_start(out=wkv_raw[:, 2 * u : 2 * u + 2, :], in_=wkv_rows[:, 2 * u : 2 * u + 2, :])
+        x_rows = x.rearrange("(pair r p) d -> pair p r d", r=2, p=P)
+        wk_rows = wk_up.rearrange("(h p) c -> p h c", p=P)
+        wv_rows = wv_up.rearrange("(h p) c -> p h c", p=P)
+
+        wkv_pieces = [load_piece([D], wkv_rows[:, t, :]) for t in range(PACK)]
         bkv_bf16 = keep.tile([P, PACK], BF16)
         nc.sync.dma_start(out=bkv_bf16[:], in_=bkv_down.rearrange("(p t) -> p t", t=PACK))
 
-        x_raw = keep.tile([P, S_TILES, D], BF16)
-        x_rows = x.rearrange("(j p) d -> p j d", p=P)
-        wk_raw = keep.tile([P, HEADS, CKV], BF16)
-        wk_rows = wk_up.rearrange("(h p) c -> p h c", p=P)
-        wv_raw = keep.tile([P, HEADS, CKV], BF16)
-        wv_rows = wv_up.rearrange("(h p) c -> p h c", p=P)
+        x_pieces = {}
+        wk_pieces = {}
+        wv_pieces = {}
 
-        def load_x_half(half):
-            for j in range(half * TILES, (half + 1) * TILES, 2):
-                nc.sync.dma_start(out=x_raw[:, j : j + 2, :], in_=x_rows[:, j : j + 2, :])
+        def load_x(pair):
+            for g2 in range(2):
+                x_pieces[pair, g2] = load_piece(
+                    [2, D // 2], x_rows[pair][:, :, g2 * D // 2 : (g2 + 1) * D // 2]
+                )
 
         def load_up_weights(q):
             heads = slice(q * CHUNK_HEADS, (q + 1) * CHUNK_HEADS)
-            nc.sync.dma_start(out=wk_raw[:, heads, :], in_=wk_rows[:, heads, :])
-            nc.sync.dma_start(out=wv_raw[:, heads, :], in_=wv_rows[:, heads, :])
+            wk_pieces[q] = load_piece([CHUNK_HEADS, CKV], wk_rows[:, heads, :])
+            wv_pieces[q] = load_piece([CHUNK_HEADS, CKV], wv_rows[:, heads, :])
 
-        load_x_half(0)
+        load_x(0)
+        load_x(1)
         load_up_weights(0)
         bk_bf16 = keep.tile([P, HEADS], BF16)
         with nc.allow_non_contiguous_dma(reason="a 4 KiB bias, one element to a partition"):
@@ -106,14 +91,16 @@ def tile_selfattention_pa_kernel(
         nc.gpsimd.tensor_copy(out=tables[:, :, 1, HALF_DIM:], in_=sin_raw[:, :, :HALF_DIM])
         bv_all = keep.tile([P, E], BF16)
         nc.sync.dma_start(out=bv_all[:], in_=bv_up.partition_broadcast(P))
-        for q in range(1, CHUNKS):
-            load_up_weights(q)
-        load_x_half(1)
+        load_up_weights(1)
+        load_x(2)
+        load_up_weights(2)
+        load_x(3)
+        load_up_weights(3)
 
-        wkv_codes = keep.tile([P, D_PASSES, CKV], U32, align_bytes=64)
-        wkv_scales = keep.tile([P, D_PASSES, CKV], U8, align_bytes=64)
-        x_codes = keep.tile([P, D_PASSES, S], U32, align_bytes=64)
-        x_scales = keep.tile([P, D_PASSES, S], U8, align_bytes=64)
+        wkv_codes = keep.tile([P, PACK, D_PASSES, P], U32, align_bytes=64)
+        wkv_scales = keep.tile([P, PACK, D_PASSES, P], U8, align_bytes=64)
+        x_codes = keep.tile([P, PAIRS, D_PASSES, PAIR], U32, align_bytes=64)
+        x_scales = keep.tile([P, PAIRS, D_PASSES, PAIR], U8, align_bytes=64)
         c_codes = keep.tile([P, S], U32, align_bytes=64)
         c_scales = keep.tile([P, S], U8, align_bytes=64)
         wk_codes = keep.tile([P, E], U32, align_bytes=64)
@@ -121,72 +108,116 @@ def tile_selfattention_pa_kernel(
         wv_codes = keep.tile([P, E], U32, align_bytes=64)
         wv_scales = keep.tile([P, E], U8, align_bytes=64)
 
-        wkv_words = wkv_raw[:].bitcast(F32)
-        x_words = x_raw[:].bitcast(F32)
-        wk_words = wk_raw[:].bitcast(F32)
-        wv_words = wv_raw[:].bitcast(F32)
-
-        def quantise_wkv(g, copies):
-            quantise_rows(
-                nc, banks, stage, identity, copies,
-                wkv_words[:, :, g * WORDS : (g + 1) * WORDS], wkv_codes[:, g, :], wkv_scales[:, g, :],
-            )
-
-        def quantise_x(first_tile, tiles, g, copies):
-            cols = slice(first_tile * P, (first_tile + tiles) * P)
-            quantise_rows(
-                nc, banks, stage, identity, copies,
-                x_words[:, first_tile : first_tile + tiles, g * WORDS : (g + 1) * WORDS],
-                x_codes[:, g, cols], x_scales[:, g, cols],
-            )
-
-        def quantise_wk(q, copies):
-            cols = slice(q * BANK, (q + 1) * BANK)
-            quantise_rows(
-                nc, banks, stage, identity, copies,
-                wk_words[:, q * CHUNK_HEADS : (q + 1) * CHUNK_HEADS, :],
-                wk_codes[:, cols], wk_scales[:, cols],
-            )
-
-        def quantise_wv(q, copies):
-            cols = slice(q * BANK, (q + 1) * BANK)
-            quantise_rows(
-                nc, banks, stage, identity, copies,
-                wv_words[:, q * CHUNK_HEADS : (q + 1) * CHUNK_HEADS, :],
-                wv_codes[:, cols], wv_scales[:, cols],
-            )
-
         bkv = keep.tile([P, PACK], F32)
         bk = keep.tile([P, HEADS], F32)
-        c_rows = keep.tile([P, S_HALVES, PACK, BANK], BF16)
 
-        def compress(half, t):
-            pos = slice(half * BANK, (half + 1) * BANK)
-            rows = slice(t * P, (t + 1) * P)
-            c_bank = banks.tile([P, BANK], F32, tag="for_scalar")
-            for g in range(D_PASSES):
-                nc.tensor.matmul_mx(
-                    out=c_bank[:],
-                    lhsT=wkv_codes[:, g, rows].bitcast(FP8X4),
-                    lhsT_scale=wkv_scales[:, g, rows],
-                    rhs=x_codes[:, g, pos].bitcast(FP8X4),
-                    rhs_scale=x_scales[:, g, pos],
-                    start=(g == 0),
-                    stop=(g == D_PASSES - 1),
+        def turn(row_passes, copies):
+            grouped = stage.tile([P, BANK, PACK], BF16, tag="grouped", align_bytes=64)
+            grouped_words = grouped[:].bitcast(F32)
+            for b in range(2):
+                bank = banks.tile([P, 2, 2, P], F32, tag="turned", bufs=4)
+                for r in range(2):
+                    for u in range(2):
+                        nc.tensor.transpose(
+                            bank[:, r, u, :], row_passes[2 * b + r][:, u:WORDS:2], identity[:]
+                        )
+                copies[b](
+                    out=grouped_words[:, b * PAIR : (b + 1) * PAIR, :].rearrange(
+                        "p (r row) u -> p r row u", r=2
+                    ),
+                    in_=bank[:].rearrange("p r u row -> p r row u"),
                 )
-            nc.scalar.activation(
-                out=c_rows[:, half, t, :], in_=c_bank[:], func=IDENTITY, bias=bkv[:, t : t + 1],
-                scale=1.0,
+            return grouped
+
+        def quantise(grouped, codes, scales):
+            nc.vector.quantize_mx(
+                out=codes.bitcast(FP8X4), scales=scales,
+                in_=grouped[:].rearrange("p row t -> p (row t)"),
             )
 
-        def quantise_c(half):
-            pos = slice(half * BANK, (half + 1) * BANK)
-            c_grouped = stage.tile([P, BANK, PACK], BF16, tag="grouped", align_bytes=64)
-            nc.vector.tensor_copy(out=c_grouped[:], in_=c_rows[:, half].rearrange("p t s -> p s t"))
+        def piece_wkv(t):
+            words = wkv_pieces[t][:].bitcast(F32)
+            passes = [words[:, g * WORDS : (g + 1) * WORDS] for g in range(D_PASSES)]
+            return (
+                passes,
+                wkv_codes[:, t].rearrange("p g row -> p (g row)"),
+                wkv_scales[:, t].rearrange("p g row -> p (g row)"),
+            )
+
+        def piece_x(pair, g2):
+            words = x_pieces[pair, g2][:].bitcast(F32)
+            passes = [words[:, r, g * WORDS : (g + 1) * WORDS] for g in range(2) for r in range(2)]
+            gs = slice(2 * g2, 2 * g2 + 2)
+            return (
+                passes,
+                x_codes[:, pair, gs, :].rearrange("p g row -> p (g row)"),
+                x_scales[:, pair, gs, :].rearrange("p g row -> p (g row)"),
+            )
+
+        def piece_up(pieces, codes, scales, q):
+            words = pieces[q][:].bitcast(F32)
+            cols = slice(q * BANK, (q + 1) * BANK)
+            return [words[:, i, :] for i in range(CHUNK_HEADS)], codes[:, cols], scales[:, cols]
+
+        def piece_wk(q):
+            return piece_up(wk_pieces, wk_codes, wk_scales, q)
+
+        def piece_wv(q):
+            return piece_up(wv_pieces, wv_codes, wv_scales, q)
+
+        unfinished = []
+
+        def finish():
+            for grouped, codes, scales in unfinished:
+                quantise(grouped, codes, scales)
+            unfinished.clear()
+
+        def prepare(piece, copies):
+            row_passes, codes, scales = piece
+            grouped = turn(row_passes, copies)
+            finish()
+            unfinished.append((grouped, codes, scales))
+
+        c_rows = {}
+        c_grouped = {}
+
+        def compress(pair, t2):
+            if t2 == 0:
+                c_rows[pair] = stage.tile([P, PACK, PAIR], BF16, tag="c_rows", name="c_rows")
+            c_bank = banks.tile([P, 2, PAIR], F32, tag="for_scalar")
+            for i in range(2):
+                t = 2 * t2 + i
+                for g in range(D_PASSES):
+                    nc.tensor.matmul_mx(
+                        out=c_bank[:, i, :],
+                        lhsT=wkv_codes[:, t, g, :].bitcast(FP8X4),
+                        lhsT_scale=wkv_scales[:, t, g, :],
+                        rhs=x_codes[:, pair, g, :].bitcast(FP8X4),
+                        rhs_scale=x_scales[:, pair, g, :],
+                        start=(g == 0),
+                        stop=(g == D_PASSES - 1),
+                    )
+            for i in range(2):
+                t = 2 * t2 + i
+                nc.scalar.activation(
+                    out=c_rows[pair][:, t, :], in_=c_bank[:, i, :], func=IDENTITY,
+                    bias=bkv[:, t : t + 1], scale=1.0,
+                )
+
+        def group_c(pair):
+            c_grouped[pair] = stage.tile(
+                [P, PAIR, PACK], BF16, tag="c_grouped", name="c_grouped", align_bytes=64
+            )
+            nc.vector.tensor_copy(
+                out=c_grouped[pair][:], in_=c_rows[pair][:].rearrange("p t s -> p s t")
+            )
+
+        def quantise_c(pair):
+            pos = slice(pair * PAIR, (pair + 1) * PAIR)
             nc.vector.quantize_mx(
                 out=c_codes[:, pos].bitcast(FP8X4),
                 scales=c_scales[:, pos],
-                in_=c_grouped[:].rearrange("p s t -> p (s t)"),
+                in_=c_grouped[pair][:].rearrange("p s t -> p (s t)"),
             )
 
         def project_key_head(half, h):
@@ -208,10 +239,10 @@ def tile_selfattention_pa_kernel(
             )
             return kT
 
-        def project_values(j, q, v_rows):
+        def project_values(j, q, v_rows, through_scalar):
             pos = slice(j * P, (j + 1) * P)
             cols = slice(q * BANK, (q + 1) * BANK)
-            v_bank = banks.tile([P, BANK], F32, tag="for_vector")
+            v_bank = banks.tile([P, BANK], F32, tag="values")
             nc.tensor.matmul_mx(
                 out=v_bank[:],
                 lhsT=c_codes[:, pos].bitcast(FP8X4),
@@ -221,7 +252,11 @@ def tile_selfattention_pa_kernel(
                 start=True,
                 stop=True,
             )
-            nc.vector.tensor_tensor(out=v_rows, in0=v_bank[:], in1=bv_all[:, cols], op=ADD)
+            if through_scalar:
+                nc.scalar.copy(out=v_rows, in_=v_bank[:])
+                nc.gpsimd.tensor_tensor(out=v_rows, in0=v_rows, in1=bv_all[:, cols], op=ADD)
+            else:
+                nc.vector.tensor_tensor(out=v_rows, in0=v_bank[:], in1=bv_all[:, cols], op=ADD)
 
         def rope_products(half, kT, products):
             k_bank = banks.tile([P, TILES, HEAD_DIM], F32, tag="turned", bufs=4)
@@ -234,72 +269,92 @@ def tile_selfattention_pa_kernel(
                 op=MULT,
             )
 
-        def rope_sums(products):
+        def rope_sums(products, rows):
             nc.gpsimd.tensor_tensor(
-                out=products[:, 0, :, :, :HALF_DIM],
+                out=rows[:, :, :, :HALF_DIM],
                 in0=products[:, 0, :, :, :HALF_DIM],
                 in1=products[:, 1, :, :, HALF_DIM:],
                 op=SUBTRACT,
             )
             nc.gpsimd.tensor_tensor(
-                out=products[:, 0, :, :, HALF_DIM:],
+                out=rows[:, :, :, HALF_DIM:],
                 in0=products[:, 0, :, :, HALF_DIM:],
                 in1=products[:, 1, :, :, :HALF_DIM],
                 op=ADD,
             )
 
-        nc.vector.tensor_copy(out=bkv[:], in_=bkv_bf16[:])
         scalar_only = (nc.scalar.copy, nc.scalar.copy)
         shared = (nc.scalar.copy, nc.vector.tensor_copy)
-        for g in range(D_PASSES):
-            quantise_wkv(g, shared)
-        for first_tile in range(0, TILES, 2):
-            for g in range(D_PASSES):
-                quantise_x(first_tile, 2, g, scalar_only)
-        quantise_wv(0, shared)
-        quantise_wk(0, shared)
-        nc.vector.tensor_copy(out=bk[:], in_=bk_bf16[:])
         for t in range(PACK):
-            compress(0, t)
+            prepare(piece_wkv(t), shared if t % 2 == 1 else scalar_only)
+        nc.vector.tensor_copy(out=bkv[:], in_=bkv_bf16[:])
+        prepare(piece_x(0, 0), scalar_only)
+        prepare(piece_x(0, 1), shared)
+        prepare(piece_x(1, 0), scalar_only)
+        compress(0, 0)
+        compress(0, 1)
+        prepare(piece_x(1, 1), shared)
+        group_c(0)
+        prepare(piece_wk(0), scalar_only)
         quantise_c(0)
+        compress(1, 0)
+        compress(1, 1)
+        nc.vector.tensor_copy(out=bk[:], in_=bk_bf16[:])
+        prepare(piece_wv(0), scalar_only)
+        group_c(1)
+        finish()
+        quantise_c(1)
 
-        later = []
-        for q in range(1, CHUNKS):
-            later.append((quantise_wk, (q, scalar_only)))
-            later.append((quantise_wv, (q, scalar_only)))
-        for g in range(D_PASSES):
-            later.append((quantise_x, (TILES, TILES, g, scalar_only)))
-        for t in range(PACK):
-            later.append((compress, (1, t)))
-        later.append((quantise_c, (1,)))
+        with_projections = {
+            5: ((compress, (2, 0)),),
+            6: ((compress, (2, 1)),),
+            7: ((group_c, (2,)),),
+            8: ((quantise_c, (2,)), (compress, (3, 0))),
+            9: ((compress, (3, 1)),),
+            10: ((group_c, (3,)),),
+            11: ((quantise_c, (3,)),),
+        }
+        pieces = {
+            0: piece_wk(1), 1: piece_wv(1), 2: piece_x(2, 0), 3: piece_x(2, 1), 4: piece_wk(2),
+            5: piece_wv(2), 6: piece_x(3, 0), 7: piece_x(3, 1), 13: piece_wk(3), 16: piece_wv(3),
+        }
 
-        steps = [(half, h) for half in range(S_HALVES) for h in range(HEADS)]
-        kT_next = project_key_head(*steps[0])
-        for step, (half, h) in enumerate(steps):
-            q, i = divmod(h, CHUNK_HEADS)
+        blocks = [(0, 0), (0, 1), (0, 2), (1, 0), (1, 1), (1, 2), (0, 3), (1, 3)]
+        steps = [(half, q, i) for half, q in blocks for i in range(CHUNK_HEADS)]
+        kT_next = project_key_head(0, 0)
+        for step, (half, q, i) in enumerate(steps):
             j = half * TILES + i
-            if h % 2 == 0:
+            if i == 0:
+                k_rows = results.tile([P, TILES, CHUNK_HEADS, HEAD_DIM], F32, tag="k_rows")
+            if i % 2 == 0:
                 products = results.tile([P, 2, TILES, 2, HEAD_DIM], F32, tag="products")
-                v_rows = results.tile([P, 2, BANK], F32, tag="v_rows")
+                v_rows = results.tile([P, 2, BANK], F32, tag="v_rows", bufs=4)
+            finish()
+            for work, arguments in with_projections.get(step, ()):
+                work(*arguments)
             kT = kT_next
             if step + 1 < len(steps):
-                kT_next = project_key_head(*steps[step + 1])
-            project_values(j, q, v_rows[:, h % 2, :])
-            rope_products(half, kT, products[:, :, :, h % 2, :])
-            if step < len(later):
-                piece, arguments = later[step]
-                piece(*arguments)
-            if h % 2 == 1:
-                rope_sums(products)
+                next_half, next_q, next_i = steps[step + 1]
+                kT_next = project_key_head(next_half, next_q * CHUNK_HEADS + next_i)
+            project_values(j, q, v_rows[:, i % 2, :], through_scalar=(i == 1))
+            rope_products(half, kT, products[:, :, :, i % 2, :])
+            if step in pieces:
+                prepare(pieces[step], scalar_only)
+            if i % 2 == 1:
+                rope_sums(products, k_rows[:, :, i - 1 : i + 1, :])
                 nc.sync.dma_start(
                     out=out_1[
                         (j - 1) * P : (j + 1) * P, q * CHUNK_HEADS : (q + 1) * CHUNK_HEADS, :
                     ].rearrange("(r p) h d -> p r (h d)", p=P),
                     in_=v_rows[:],
                 )
+            last_block = step >= len(steps) - CHUNK_HEADS
+            if i == CHUNK_HEADS - 1 or (last_block and i % 2 == 1):
+                first = i - 1 if last_block else 0
                 nc.sync.dma_start(
-                    out=out_0[half * BANK : (half + 1) * BANK, h - 1 : h + 1, :].rearrange(
-                        "(j p) h d -> p j h d", p=P
-                    ),
-                    in_=products[:, 0],
+                    out=out_0[
+                        half * BANK : (half + 1) * BANK,
+                        q * CHUNK_HEADS + first : q * CHUNK_HEADS + i + 1, :,
+                    ].rearrange("(j p) h d -> p j h d", p=P),
+                    in_=k_rows[:, :, first : i + 1, :],
                 )

@@ -47,6 +47,14 @@ def tile_selfattention_pa_kernel(
 
         identity = keep.tile([P, P], F32)
         make_identity(nc, identity[:])
+        identity_bf16 = keep.tile([P, P], BF16)
+        nc.gpsimd.tensor_copy(out=identity_bf16[:], in_=identity[:])
+        bk_rows = keep.tile([P, HEAD_DIM], BF16)
+        bv_row = keep.tile([P, E], BF16)
+        ones = keep.tile([P, P], BF16)
+        nc.vector.memset(bk_rows[:], 0.0)
+        nc.vector.memset(bv_row[:], 0.0)
+        nc.vector.memset(ones[:], 1.0)
 
         def load_piece(shape, source):
             piece = raw.tile([P] + shape, BF16, tag="piece", name="piece")
@@ -54,13 +62,15 @@ def tile_selfattention_pa_kernel(
             return piece
 
         wkv_rows = wkv_down.rearrange("(p t) d -> p t d", t=PACK)
-        x_rows = x.rearrange("(pair r p) d -> pair p r d", r=2, p=P)
+        x_rows = x.rearrange("(p j) d -> p j d", j=S_TILES)
         wk_rows = wk_up.rearrange("(h p) c -> p h c", p=P)
         wv_rows = wv_up.rearrange("(h p) c -> p h c", p=P)
 
         wkv_pieces = [load_piece([D], wkv_rows[:, t, :]) for t in range(PACK)]
         bkv_bf16 = keep.tile([P, PACK], BF16)
         nc.sync.dma_start(out=bkv_bf16[:], in_=bkv_down.rearrange("(p t) -> p t", t=PACK))
+        nc.sync.dma_start(out=bk_rows[:HEADS, :], in_=bk_up.rearrange("(h d) -> h d", d=HEAD_DIM))
+        nc.sync.dma_start(out=bv_row[:1, :], in_=bv_up.rearrange("(o e) -> o e", o=1))
 
         x_pieces = {}
         wk_pieces = {}
@@ -69,7 +79,7 @@ def tile_selfattention_pa_kernel(
         def load_x(pair):
             for g2 in range(2):
                 x_pieces[pair, g2] = load_piece(
-                    [2, D // 2], x_rows[pair][:, :, g2 * D // 2 : (g2 + 1) * D // 2]
+                    [2, D // 2], x_rows[:, 2 * pair : 2 * pair + 2, g2 * D // 2 : (g2 + 1) * D // 2]
                 )
 
         def load_up_weights(q):
@@ -80,17 +90,12 @@ def tile_selfattention_pa_kernel(
         load_x(0)
         load_x(1)
         load_up_weights(0)
-        bk_bf16 = keep.tile([P, HEADS], BF16)
-        with nc.allow_non_contiguous_dma(reason="a 4 KiB bias, one element to a partition"):
-            nc.sync.dma_start(out=bk_bf16[:], in_=bk_up.rearrange("(h d) -> d h", d=HEAD_DIM))
-        tables = keep.tile([P, S_TILES, 2, HEAD_DIM], BF16)
+        tables = keep.tile([P, 2, S_TILES, HEAD_DIM], BF16)
         sin_raw = keep.tile([P, S_TILES, HEAD_DIM], BF16)
-        nc.sync.dma_start(out=tables[:, :, 0, :], in_=rope_cos.rearrange("(j p) d -> p j d", p=P))
-        nc.sync.dma_start(out=sin_raw[:], in_=rope_sin.rearrange("(j p) d -> p j d", p=P))
-        nc.gpsimd.tensor_copy(out=tables[:, :, 1, :HALF_DIM], in_=sin_raw[:, :, HALF_DIM:])
-        nc.gpsimd.tensor_copy(out=tables[:, :, 1, HALF_DIM:], in_=sin_raw[:, :, :HALF_DIM])
-        bv_all = keep.tile([P, E], BF16)
-        nc.sync.dma_start(out=bv_all[:], in_=bv_up.partition_broadcast(P))
+        nc.sync.dma_start(out=tables[:, 0], in_=rope_cos.rearrange("(p j) d -> p j d", j=S_TILES))
+        nc.sync.dma_start(out=sin_raw[:], in_=rope_sin.rearrange("(p j) d -> p j d", j=S_TILES))
+        nc.gpsimd.tensor_copy(out=tables[:, 1, :, :HALF_DIM], in_=sin_raw[:, :, HALF_DIM:])
+        nc.gpsimd.tensor_copy(out=tables[:, 1, :, HALF_DIM:], in_=sin_raw[:, :, :HALF_DIM])
         load_up_weights(1)
         load_x(2)
         load_up_weights(2)
@@ -110,6 +115,18 @@ def tile_selfattention_pa_kernel(
 
         bkv = keep.tile([P, PACK], F32)
         bk = keep.tile([P, HEADS], F32)
+        bv_all = keep.tile([P, E], BF16)
+
+        def spread_key_bias():
+            bank = banks.tile([P, P], BF16, tag="values")
+            nc.tensor.transpose(bank[:], bk_rows[:], identity_bf16[:])
+            nc.vector.tensor_copy(out=bk[:], in_=bank[:, :HEADS])
+
+        def spread_value_bias(q, copy):
+            cols = slice(q * BANK, (q + 1) * BANK)
+            bank = banks.tile([P, BANK], F32, tag="values")
+            nc.tensor.matmul(bank[:], ones[:], bv_row[:, cols], start=True, stop=True)
+            copy(out=bv_all[:, cols], in_=bank[:])
 
         def turn(row_passes, copies):
             grouped = stage.tile([P, BANK, PACK], BF16, tag="grouped", align_bytes=64)
@@ -265,7 +282,7 @@ def tile_selfattention_pa_kernel(
             nc.vector.tensor_tensor(
                 out=products,
                 in0=k_bank[:].unsqueeze(1).to_broadcast([P, 2, TILES, HEAD_DIM]),
-                in1=tables[:, half * TILES : (half + 1) * TILES].rearrange("p j c d -> p c j d"),
+                in1=tables[:, :, half * TILES : (half + 1) * TILES, :],
                 op=MULT,
             )
 
@@ -288,6 +305,9 @@ def tile_selfattention_pa_kernel(
         for t in range(PACK):
             prepare(piece_wkv(t), shared if t % 2 == 1 else scalar_only)
         nc.vector.tensor_copy(out=bkv[:], in_=bkv_bf16[:])
+        spread_key_bias()
+        for q in range(CHUNKS):
+            spread_value_bias(q, nc.vector.tensor_copy if q % 2 == 0 else nc.scalar.copy)
         prepare(piece_x(0, 0), scalar_only)
         prepare(piece_x(0, 1), shared)
         prepare(piece_x(1, 0), scalar_only)
@@ -299,7 +319,6 @@ def tile_selfattention_pa_kernel(
         quantise_c(0)
         compress(1, 0)
         compress(1, 1)
-        nc.vector.tensor_copy(out=bk[:], in_=bk_bf16[:])
         prepare(piece_wv(0), scalar_only)
         group_c(1)
         finish()
@@ -321,6 +340,8 @@ def tile_selfattention_pa_kernel(
 
         blocks = [(0, 0), (0, 1), (0, 2), (1, 0), (1, 1), (1, 2), (0, 3), (1, 3)]
         steps = [(half, q, i) for half, q in blocks for i in range(CHUNK_HEADS)]
+        k_out = out_0.rearrange("(p j) h d -> p j (h d)", j=S_TILES)
+        v_out = out_1.rearrange("(p j) h d -> p j (h d)", j=S_TILES)
         kT_next = project_key_head(0, 0)
         for step, (half, q, i) in enumerate(steps):
             j = half * TILES + i
@@ -343,18 +364,16 @@ def tile_selfattention_pa_kernel(
             if i % 2 == 1:
                 rope_sums(products, k_rows[:, :, i - 1 : i + 1, :])
                 nc.sync.dma_start(
-                    out=out_1[
-                        (j - 1) * P : (j + 1) * P, q * CHUNK_HEADS : (q + 1) * CHUNK_HEADS, :
-                    ].rearrange("(r p) h d -> p r (h d)", p=P),
+                    out=v_out[:, j - 1 : j + 1, q * BANK : (q + 1) * BANK],
                     in_=v_rows[:],
                 )
             last_block = step >= len(steps) - CHUNK_HEADS
             if i == CHUNK_HEADS - 1 or (last_block and i % 2 == 1):
                 first = i - 1 if last_block else 0
                 nc.sync.dma_start(
-                    out=out_0[
-                        half * BANK : (half + 1) * BANK,
-                        q * CHUNK_HEADS + first : q * CHUNK_HEADS + i + 1, :,
-                    ].rearrange("(j p) h d -> p j h d", p=P),
-                    in_=k_rows[:, :, first : i + 1, :],
+                    out=k_out[
+                        :, half * TILES : (half + 1) * TILES,
+                        (q * CHUNK_HEADS + first) * HEAD_DIM : (q * CHUNK_HEADS + i + 1) * HEAD_DIM,
+                    ],
+                    in_=k_rows[:, :, first : i + 1, :].rearrange("p j h d -> p j (h d)"),
                 )

@@ -23,6 +23,7 @@ S, D, CKV, HEADS, HEAD_DIM = 1024, 2048, 512, 16, 128
 E = HEADS * HEAD_DIM
 HALF_DIM = HEAD_DIM // 2
 S_TILES = S // P
+S_HALVES = S // BANK
 TILES = BANK // P
 PAIR = 2 * P
 PAIRS = S // PAIR
@@ -49,12 +50,14 @@ def tile_selfattention_pa_kernel(
         make_identity(nc, identity[:])
         identity_bf16 = keep.tile([P, P], BF16)
         nc.gpsimd.tensor_copy(out=identity_bf16[:], in_=identity[:])
+        exchange = keep.tile([P, P], F32)
+        nc.gpsimd.tensor_copy(out=exchange[:, :HALF_DIM], in_=identity[:, HALF_DIM:])
+        nc.gpsimd.tensor_copy(out=exchange[:, HALF_DIM:], in_=identity[:, :HALF_DIM])
+        sign = keep.tile([P, 1], F32)
+        nc.gpsimd.memset(sign[:], 1.0)
+        nc.gpsimd.memset(sign[HALF_DIM:], -1.0)
         bk_rows = keep.tile([P, HEAD_DIM], BF16)
-        bv_row = keep.tile([P, E], BF16)
-        ones = keep.tile([P, P], BF16)
         nc.vector.memset(bk_rows[:], 0.0)
-        nc.vector.memset(bv_row[:], 0.0)
-        nc.vector.memset(ones[:], 1.0)
 
         def load_piece(shape, source):
             piece = raw.tile([P] + shape, BF16, tag="piece", name="piece")
@@ -70,11 +73,11 @@ def tile_selfattention_pa_kernel(
         bkv_bf16 = keep.tile([P, PACK], BF16)
         nc.sync.dma_start(out=bkv_bf16[:], in_=bkv_down.rearrange("(p t) -> p t", t=PACK))
         nc.sync.dma_start(out=bk_rows[:HEADS, :], in_=bk_up.rearrange("(h d) -> h d", d=HEAD_DIM))
-        nc.sync.dma_start(out=bv_row[:1, :], in_=bv_up.rearrange("(o e) -> o e", o=1))
 
         x_pieces = {}
         wk_pieces = {}
         wv_pieces = {}
+        bv_all = keep.tile([P, E], BF16)
 
         def load_x(pair):
             for g2 in range(2):
@@ -87,6 +90,9 @@ def tile_selfattention_pa_kernel(
             wk_pieces[q] = load_piece([CHUNK_HEADS, CKV], wk_rows[:, heads, :])
             wv_pieces[q] = load_piece([CHUNK_HEADS, CKV], wv_rows[:, heads, :])
 
+        def load_value_bias(cols):
+            nc.sync.dma_start(out=bv_all[:, cols], in_=bv_up[cols].partition_broadcast(P))
+
         load_x(0)
         load_x(1)
         load_up_weights(0)
@@ -96,11 +102,13 @@ def tile_selfattention_pa_kernel(
         nc.sync.dma_start(out=sin_raw[:], in_=rope_sin.rearrange("(p j) d -> p j d", j=S_TILES))
         nc.gpsimd.tensor_copy(out=tables[:, 1, :, :HALF_DIM], in_=sin_raw[:, :, HALF_DIM:])
         nc.gpsimd.tensor_copy(out=tables[:, 1, :, HALF_DIM:], in_=sin_raw[:, :, :HALF_DIM])
+        load_value_bias(slice(0, BANK))
         load_up_weights(1)
-        load_x(2)
+        load_value_bias(slice(BANK, E))
         load_up_weights(2)
-        load_x(3)
+        load_x(2)
         load_up_weights(3)
+        load_x(3)
 
         wkv_codes = keep.tile([P, PACK, D_PASSES, P], U32, align_bytes=64)
         wkv_scales = keep.tile([P, PACK, D_PASSES, P], U8, align_bytes=64)
@@ -115,18 +123,25 @@ def tile_selfattention_pa_kernel(
 
         bkv = keep.tile([P, PACK], F32)
         bk = keep.tile([P, HEADS], F32)
-        bv_all = keep.tile([P, E], BF16)
+        tables_turned = keep.tile([P, 2, S], BF16)
 
         def spread_key_bias():
             bank = banks.tile([P, P], BF16, tag="values")
             nc.tensor.transpose(bank[:], bk_rows[:], identity_bf16[:])
             nc.vector.tensor_copy(out=bk[:], in_=bank[:, :HEADS])
 
-        def spread_value_bias(q, copy):
-            cols = slice(q * BANK, (q + 1) * BANK)
-            bank = banks.tile([P, BANK], F32, tag="values")
-            nc.tensor.matmul(bank[:], ones[:], bv_row[:, cols], start=True, stop=True)
-            copy(out=bv_all[:, cols], in_=bank[:])
+        def turn_tables(plane, half):
+            bank = banks.tile([P, TILES, P], BF16, tag="values")
+            for jj in range(TILES):
+                nc.tensor.transpose(
+                    bank[:, jj, :], tables[:, plane, half * TILES + jj, :], identity_bf16[:]
+                )
+            nc.scalar.activation(
+                out=tables_turned[:, plane, half * BANK : (half + 1) * BANK],
+                in_=bank[:].rearrange("p j row -> p (j row)"),
+                func=IDENTITY,
+                scale=1.0 if plane == 0 else sign[:, :1],
+            )
 
         def turn(row_passes, copies):
             grouped = stage.tile([P, BANK, PACK], BF16, tag="grouped", align_bytes=64)
@@ -201,7 +216,7 @@ def tile_selfattention_pa_kernel(
         def compress(pair, t2):
             if t2 == 0:
                 c_rows[pair] = stage.tile([P, PACK, PAIR], BF16, tag="c_rows", name="c_rows")
-            c_bank = banks.tile([P, 2, PAIR], F32, tag="for_scalar")
+            c_bank = banks.tile([P, 2, PAIR], F32, tag="turned", bufs=4)
             for i in range(2):
                 t = 2 * t2 + i
                 for g in range(D_PASSES):
@@ -237,12 +252,23 @@ def tile_selfattention_pa_kernel(
                 in_=c_grouped[pair][:].rearrange("p s t -> p (s t)"),
             )
 
-        def project_key_head(half, h):
+        blocks = [(half, q) for half in range(S_HALVES) for q in range(CHUNKS)]
+        steps = [(half, q, i) for half, q in blocks for i in range(CHUNK_HEADS)]
+
+        def summed_by_tensor(i):
+            return i % 2 == 1
+
+        def through_scalar(i):
+            return i % 2 == 1
+
+        def project_keys(step):
+            half, q, i = steps[step]
+            h = q * CHUNK_HEADS + i
             pos = slice(half * BANK, (half + 1) * BANK)
             cols = slice(h * HEAD_DIM, (h + 1) * HEAD_DIM)
-            kT_bank = banks.tile([P, BANK], F32, tag="for_scalar")
+            k_bank = banks.tile([P, BANK], F32, tag="keys")
             nc.tensor.matmul_mx(
-                out=kT_bank[:],
+                out=k_bank[:],
                 lhsT=wk_codes[:, cols].bitcast(FP8X4),
                 lhsT_scale=wk_scales[:, cols],
                 rhs=c_codes[:, pos].bitcast(FP8X4),
@@ -250,13 +276,17 @@ def tile_selfattention_pa_kernel(
                 start=True,
                 stop=True,
             )
+            if summed_by_tensor(i):
+                return k_bank
             kT = stage.tile([P, BANK], F32, tag="kT")
             nc.scalar.activation(
-                out=kT[:], in_=kT_bank[:], func=IDENTITY, bias=bk[:, h : h + 1], scale=1.0
+                out=kT[:], in_=k_bank[:], func=IDENTITY, bias=bk[:, h : h + 1], scale=1.0
             )
             return kT
 
-        def project_values(j, q, v_rows, through_scalar):
+        def project_values(step):
+            half, q, i = steps[step]
+            j = half * TILES + i
             pos = slice(j * P, (j + 1) * P)
             cols = slice(q * BANK, (q + 1) * BANK)
             v_bank = banks.tile([P, BANK], F32, tag="values")
@@ -269,48 +299,79 @@ def tile_selfattention_pa_kernel(
                 start=True,
                 stop=True,
             )
-            if through_scalar:
-                nc.scalar.copy(out=v_rows, in_=v_bank[:])
-                nc.gpsimd.tensor_tensor(out=v_rows, in0=v_rows, in1=bv_all[:, cols], op=ADD)
-            else:
-                nc.vector.tensor_tensor(out=v_rows, in0=v_bank[:], in1=bv_all[:, cols], op=ADD)
+            return v_bank
 
-        def rope_products(half, kT, products):
-            k_bank = banks.tile([P, TILES, HEAD_DIM], F32, tag="turned", bufs=4)
+        def finish_values(step, v_bank, v_rows):
+            half, q, i = steps[step]
+            bias = bv_all[:, q * BANK : (q + 1) * BANK]
+            if through_scalar(i):
+                nc.scalar.copy(out=v_rows, in_=v_bank[:])
+                nc.gpsimd.tensor_tensor(out=v_rows, in0=v_rows, in1=bias, op=ADD)
+            else:
+                nc.vector.tensor_tensor(out=v_rows, in0=v_bank[:], in1=bias, op=ADD)
+
+        def turn_back(kT):
+            bank = banks.tile([P, TILES, HEAD_DIM], F32, tag="turned", bufs=4)
             for jj in range(TILES):
-                nc.tensor.transpose(k_bank[:, jj, :], kT[:, jj * P : (jj + 1) * P], identity[:])
+                nc.tensor.transpose(bank[:, jj, :], kT[:, jj * P : (jj + 1) * P], identity[:])
+            return bank
+
+        def rope_by_gpsimd(half, bank, rows):
+            products = results.tile([P, 2, TILES, HEAD_DIM], F32, tag="products")
             nc.vector.tensor_tensor(
-                out=products,
-                in0=k_bank[:].unsqueeze(1).to_broadcast([P, 2, TILES, HEAD_DIM]),
+                out=products[:],
+                in0=bank[:].unsqueeze(1).to_broadcast([P, 2, TILES, HEAD_DIM]),
                 in1=tables[:, :, half * TILES : (half + 1) * TILES, :],
                 op=MULT,
             )
-
-        def rope_sums(products, rows):
             nc.gpsimd.tensor_tensor(
-                out=rows[:, :, :, :HALF_DIM],
-                in0=products[:, 0, :, :, :HALF_DIM],
-                in1=products[:, 1, :, :, HALF_DIM:],
+                out=rows[:, :, :HALF_DIM],
+                in0=products[:, 0, :, :HALF_DIM],
+                in1=products[:, 1, :, HALF_DIM:],
                 op=SUBTRACT,
             )
             nc.gpsimd.tensor_tensor(
-                out=rows[:, :, :, HALF_DIM:],
-                in0=products[:, 0, :, :, HALF_DIM:],
-                in1=products[:, 1, :, :, :HALF_DIM],
+                out=rows[:, :, HALF_DIM:],
+                in0=products[:, 0, :, HALF_DIM:],
+                in1=products[:, 1, :, :HALF_DIM],
                 op=ADD,
             )
+
+        def turned_products(half, h, k_bank):
+            products = results.tile([P, 2, BANK], F32, tag="turned_products")
+            nc.vector.scalar_tensor_tensor(
+                out=products[:],
+                in0=k_bank[:].unsqueeze(1).to_broadcast([P, 2, BANK]),
+                scalar=bk[:, h : h + 1],
+                in1=tables_turned[:, :, half * BANK : (half + 1) * BANK],
+                op0=ADD,
+                op1=MULT,
+            )
+            return products
+
+        def sum_by_tensor(products, rows):
+            bank = banks.tile([P, TILES, HEAD_DIM], F32, tag="turned", bufs=4)
+            for jj in range(TILES):
+                pos = slice(jj * P, (jj + 1) * P)
+                nc.tensor.matmul(
+                    bank[:, jj, :], products[:, 0, pos], identity[:],
+                    start=True, stop=False, is_transpose=True,
+                )
+                nc.tensor.matmul(
+                    bank[:, jj, :], products[:, 1, pos], exchange[:],
+                    start=False, stop=True, is_transpose=True,
+                )
+            nc.scalar.copy(out=rows, in_=bank[:])
 
         scalar_only = (nc.scalar.copy, nc.scalar.copy)
         shared = (nc.scalar.copy, nc.vector.tensor_copy)
         for t in range(PACK):
             prepare(piece_wkv(t), shared if t % 2 == 1 else scalar_only)
         nc.vector.tensor_copy(out=bkv[:], in_=bkv_bf16[:])
-        spread_key_bias()
-        for q in range(CHUNKS):
-            spread_value_bias(q, nc.vector.tensor_copy if q % 2 == 0 else nc.scalar.copy)
         prepare(piece_x(0, 0), scalar_only)
         prepare(piece_x(0, 1), shared)
         prepare(piece_x(1, 0), scalar_only)
+        spread_key_bias()
         compress(0, 0)
         compress(0, 1)
         prepare(piece_x(1, 1), shared)
@@ -321,59 +382,73 @@ def tile_selfattention_pa_kernel(
         compress(1, 1)
         prepare(piece_wv(0), scalar_only)
         group_c(1)
-        finish()
         quantise_c(1)
+        finish()
+        for plane in range(2):
+            for half in range(S_HALVES):
+                turn_tables(plane, half)
 
-        with_projections = {
-            5: ((compress, (2, 0)),),
-            6: ((compress, (2, 1)),),
-            7: ((group_c, (2,)),),
-            8: ((quantise_c, (2,)), (compress, (3, 0))),
-            9: ((compress, (3, 1)),),
-            10: ((group_c, (3,)),),
-            11: ((quantise_c, (3,)),),
-        }
         pieces = {
-            0: piece_wk(1), 1: piece_wv(1), 2: piece_x(2, 0), 3: piece_x(2, 1), 4: piece_wk(2),
-            5: piece_wv(2), 6: piece_x(3, 0), 7: piece_x(3, 1), 13: piece_wk(3), 16: piece_wv(3),
+            0: piece_wk(1), 1: piece_wv(1), 3: piece_wk(2), 4: piece_wv(2), 5: piece_x(2, 0),
+            6: piece_x(2, 1), 7: piece_wk(3), 8: piece_wv(3), 9: piece_x(3, 0), 10: piece_x(3, 1),
         }
+        stage_1 = {8: (2, 0), 9: (2, 1), 12: (3, 0), 13: (3, 1)}
+        grouping = {10: 2, 13: 3}
+        quantising = {11: 2, 14: 3}
 
-        blocks = [(0, 0), (0, 1), (0, 2), (1, 0), (1, 1), (1, 2), (0, 3), (1, 3)]
-        steps = [(half, q, i) for half, q in blocks for i in range(CHUNK_HEADS)]
         k_out = out_0.rearrange("(p j) h d -> p j (h d)", j=S_TILES)
         v_out = out_1.rearrange("(p j) h d -> p j (h d)", j=S_TILES)
-        kT_next = project_key_head(0, 0)
+        keys = project_keys(0)
+        v_bank = project_values(0)
+        waiting = []
+
+        def store_keys(half, q, first, count, k_rows):
+            start = (q * CHUNK_HEADS + first) * HEAD_DIM
+            nc.sync.dma_start(
+                out=k_out[
+                    :, half * TILES : (half + 1) * TILES, start : start + count * HEAD_DIM
+                ],
+                in_=k_rows[:, :, first : first + count, :].rearrange("p j h d -> p j (h d)"),
+            )
+
+        def finish_keys():
+            for step, products, k_rows in waiting:
+                half, q, i = steps[step]
+                sum_by_tensor(products, k_rows[:, :, i, :])
+                if step >= len(steps) - CHUNK_HEADS:
+                    store_keys(half, q, i - 1, 2, k_rows)
+                elif i == CHUNK_HEADS - 1:
+                    store_keys(half, q, 0, CHUNK_HEADS, k_rows)
+            waiting.clear()
+
         for step, (half, q, i) in enumerate(steps):
             j = half * TILES + i
             if i == 0:
                 k_rows = results.tile([P, TILES, CHUNK_HEADS, HEAD_DIM], F32, tag="k_rows")
             if i % 2 == 0:
-                products = results.tile([P, 2, TILES, 2, HEAD_DIM], F32, tag="products")
                 v_rows = results.tile([P, 2, BANK], F32, tag="v_rows", bufs=4)
-            finish()
-            for work, arguments in with_projections.get(step, ()):
-                work(*arguments)
-            kT = kT_next
+            finish_keys()
+            finish_values(step, v_bank, v_rows[:, i % 2, :])
+            if summed_by_tensor(i):
+                products = turned_products(half, q * CHUNK_HEADS + i, keys)
+                waiting.append((step, products, k_rows))
+            else:
+                rope_by_gpsimd(half, turn_back(keys), k_rows[:, :, i, :])
+            if step in stage_1:
+                compress(*stage_1[step])
             if step + 1 < len(steps):
-                next_half, next_q, next_i = steps[step + 1]
-                kT_next = project_key_head(next_half, next_q * CHUNK_HEADS + next_i)
-            project_values(j, q, v_rows[:, i % 2, :], through_scalar=(i == 1))
-            rope_products(half, kT, products[:, :, :, i % 2, :])
+                keys = project_keys(step + 1)
+                v_bank = project_values(step + 1)
+            if step in grouping:
+                group_c(grouping[step])
+            if step in quantising:
+                quantise_c(quantising[step])
             if step in pieces:
                 prepare(pieces[step], scalar_only)
+            else:
+                finish()
             if i % 2 == 1:
-                rope_sums(products, k_rows[:, :, i - 1 : i + 1, :])
                 nc.sync.dma_start(
-                    out=v_out[:, j - 1 : j + 1, q * BANK : (q + 1) * BANK],
-                    in_=v_rows[:],
+                    out=v_out[:, j - 1 : j + 1, q * BANK : (q + 1) * BANK], in_=v_rows[:]
                 )
-            last_block = step >= len(steps) - CHUNK_HEADS
-            if i == CHUNK_HEADS - 1 or (last_block and i % 2 == 1):
-                first = i - 1 if last_block else 0
-                nc.sync.dma_start(
-                    out=k_out[
-                        :, half * TILES : (half + 1) * TILES,
-                        (q * CHUNK_HEADS + first) * HEAD_DIM : (q * CHUNK_HEADS + i + 1) * HEAD_DIM,
-                    ],
-                    in_=k_rows[:, :, first : i + 1, :].rearrange("p j h d -> p j (h d)"),
-                )
+        finish_keys()

@@ -43,7 +43,7 @@ def tile_selfattention_pa_kernel(
         raw = pools.enter_context(tc.tile_pool(name="raw", bufs=16))
         stage = pools.enter_context(tc.tile_pool(name="stage", bufs=3))
         results = pools.enter_context(tc.tile_pool(name="results", bufs=3))
-        banks = pools.enter_context(tc.psum_pool(name="banks", bufs=2))
+        banks = pools.enter_context(tc.psum_pool(name="banks", bufs=4))
         pools.enter_context(tc.manual_schedule())
 
         identity = keep.tile([P, P], F32)
@@ -126,12 +126,12 @@ def tile_selfattention_pa_kernel(
         tables_turned = keep.tile([P, 2, S], BF16)
 
         def spread_key_bias():
-            bank = banks.tile([P, P], BF16, tag="values")
+            bank = banks.tile([P, P], BF16, tag="vector")
             nc.tensor.transpose(bank[:], bk_rows[:], identity_bf16[:])
             nc.vector.tensor_copy(out=bk[:], in_=bank[:, :HEADS])
 
         def turn_tables(plane, half):
-            bank = banks.tile([P, TILES, P], BF16, tag="values")
+            bank = banks.tile([P, TILES, P], BF16, tag="scalar")
             for jj in range(TILES):
                 nc.tensor.transpose(
                     bank[:, jj, :], tables[:, plane, half * TILES + jj, :], identity_bf16[:]
@@ -147,7 +147,8 @@ def tile_selfattention_pa_kernel(
             grouped = stage.tile([P, BANK, PACK], BF16, tag="grouped", align_bytes=64)
             grouped_words = grouped[:].bitcast(F32)
             for b in range(2):
-                bank = banks.tile([P, 2, 2, P], F32, tag="turned", bufs=4)
+                reader = "scalar" if copies[b] == nc.scalar.copy else "vector"
+                bank = banks.tile([P, 2, 2, P], F32, tag=reader)
                 for r in range(2):
                     for u in range(2):
                         nc.tensor.transpose(
@@ -216,7 +217,7 @@ def tile_selfattention_pa_kernel(
         def compress(pair, t2):
             if t2 == 0:
                 c_rows[pair] = stage.tile([P, PACK, PAIR], BF16, tag="c_rows", name="c_rows")
-            c_bank = banks.tile([P, 2, PAIR], F32, tag="turned", bufs=4)
+            c_bank = banks.tile([P, 2, PAIR], F32, tag="scalar")
             for i in range(2):
                 t = 2 * t2 + i
                 for g in range(D_PASSES):
@@ -252,21 +253,27 @@ def tile_selfattention_pa_kernel(
                 in_=c_grouped[pair][:].rearrange("p s t -> p (s t)"),
             )
 
-        blocks = [(half, q) for half in range(S_HALVES) for q in range(CHUNKS)]
-        steps = [(half, q, i) for half, q in blocks for i in range(CHUNK_HEADS)]
+        heads = [
+            (half, q, i)
+            for half in range(S_HALVES)
+            for q in range(CHUNKS)
+            for i in range(CHUNK_HEADS)
+        ]
 
-        def summed_by_tensor(i):
-            return i % 2 == 1
+        def summed_by_tensor(head):
+            half, q, i = heads[head]
+            return half == 1 and i != 0
 
-        def through_scalar(i):
-            return i % 2 == 1
+        def through_scalar(head):
+            half, q, i = heads[head]
+            return i % 2 == 1 or (half == 1 and i != 0 and head != len(heads) - 2)
 
-        def project_keys(step):
-            half, q, i = steps[step]
+        def project_keys(head):
+            half, q, i = heads[head]
             h = q * CHUNK_HEADS + i
             pos = slice(half * BANK, (half + 1) * BANK)
             cols = slice(h * HEAD_DIM, (h + 1) * HEAD_DIM)
-            k_bank = banks.tile([P, BANK], F32, tag="keys")
+            k_bank = banks.tile([P, BANK], F32, tag="vector" if summed_by_tensor(head) else "scalar")
             nc.tensor.matmul_mx(
                 out=k_bank[:],
                 lhsT=wk_codes[:, cols].bitcast(FP8X4),
@@ -276,7 +283,7 @@ def tile_selfattention_pa_kernel(
                 start=True,
                 stop=True,
             )
-            if summed_by_tensor(i):
+            if summed_by_tensor(head):
                 return k_bank
             kT = stage.tile([P, BANK], F32, tag="kT")
             nc.scalar.activation(
@@ -284,12 +291,12 @@ def tile_selfattention_pa_kernel(
             )
             return kT
 
-        def project_values(step):
-            half, q, i = steps[step]
+        def project_values(head):
+            half, q, i = heads[head]
             j = half * TILES + i
             pos = slice(j * P, (j + 1) * P)
             cols = slice(q * BANK, (q + 1) * BANK)
-            v_bank = banks.tile([P, BANK], F32, tag="values")
+            v_bank = banks.tile([P, BANK], F32, tag="scalar" if through_scalar(head) else "vector")
             nc.tensor.matmul_mx(
                 out=v_bank[:],
                 lhsT=c_codes[:, pos].bitcast(FP8X4),
@@ -301,17 +308,17 @@ def tile_selfattention_pa_kernel(
             )
             return v_bank
 
-        def finish_values(step, v_bank, v_rows):
-            half, q, i = steps[step]
+        def finish_values(head, v_bank, v_rows):
+            half, q, i = heads[head]
             bias = bv_all[:, q * BANK : (q + 1) * BANK]
-            if through_scalar(i):
+            if through_scalar(head):
                 nc.scalar.copy(out=v_rows, in_=v_bank[:])
                 nc.gpsimd.tensor_tensor(out=v_rows, in0=v_rows, in1=bias, op=ADD)
             else:
                 nc.vector.tensor_tensor(out=v_rows, in0=v_bank[:], in1=bias, op=ADD)
 
         def turn_back(kT):
-            bank = banks.tile([P, TILES, HEAD_DIM], F32, tag="turned", bufs=4)
+            bank = banks.tile([P, TILES, HEAD_DIM], F32, tag="vector")
             for jj in range(TILES):
                 nc.tensor.transpose(bank[:, jj, :], kT[:, jj * P : (jj + 1) * P], identity[:])
             return bank
@@ -350,7 +357,7 @@ def tile_selfattention_pa_kernel(
             return products
 
         def sum_by_tensor(products, rows):
-            bank = banks.tile([P, TILES, HEAD_DIM], F32, tag="turned", bufs=4)
+            bank = banks.tile([P, TILES, HEAD_DIM], F32, tag="scalar")
             for jj in range(TILES):
                 pos = slice(jj * P, (jj + 1) * P)
                 nc.tensor.matmul(
@@ -371,36 +378,34 @@ def tile_selfattention_pa_kernel(
         prepare(piece_x(0, 0), scalar_only)
         prepare(piece_x(0, 1), shared)
         prepare(piece_x(1, 0), scalar_only)
+        finish()
         spread_key_bias()
         compress(0, 0)
         compress(0, 1)
         prepare(piece_x(1, 1), shared)
+        finish()
+        prepare(piece_wk(0), shared)
         group_c(0)
-        prepare(piece_wk(0), scalar_only)
+        finish()
         quantise_c(0)
         compress(1, 0)
         compress(1, 1)
         prepare(piece_wv(0), scalar_only)
         group_c(1)
         quantise_c(1)
-        finish()
-        for plane in range(2):
-            for half in range(S_HALVES):
-                turn_tables(plane, half)
 
         pieces = {
-            0: piece_wk(1), 1: piece_wv(1), 3: piece_wk(2), 4: piece_wv(2), 5: piece_x(2, 0),
-            6: piece_x(2, 1), 7: piece_wk(3), 8: piece_wv(3), 9: piece_x(3, 0), 10: piece_x(3, 1),
+            0: (piece_wk(1), piece_wv(1)), 1: (piece_wk(2), piece_x(2, 0)),
+            2: (piece_x(2, 1), piece_wv(2)), 3: (piece_wk(3), piece_x(3, 0)),
+            4: (piece_x(3, 1), piece_wv(3)),
         }
-        stage_1 = {8: (2, 0), 9: (2, 1), 12: (3, 0), 13: (3, 1)}
-        grouping = {10: 2, 13: 3}
-        quantising = {11: 2, 14: 3}
+        stage_1 = {3: ((2, 0),), 4: ((2, 1),), 5: ((3, 0), (3, 1))}
+        grouping = {5: 2, 6: 3}
+        quantising = {5: 2, 6: 3}
+        tables_to_turn = {6: (0, 1), 7: (1, 1)}
 
         k_out = out_0.rearrange("(p j) h d -> p j (h d)", j=S_TILES)
         v_out = out_1.rearrange("(p j) h d -> p j (h d)", j=S_TILES)
-        keys = project_keys(0)
-        v_bank = project_values(0)
-        waiting = []
 
         def store_keys(half, q, first, count, k_rows):
             start = (q * CHUNK_HEADS + first) * HEAD_DIM
@@ -411,44 +416,68 @@ def tile_selfattention_pa_kernel(
                 in_=k_rows[:, :, first : first + count, :].rearrange("p j h d -> p j (h d)"),
             )
 
-        def finish_keys():
-            for step, products, k_rows in waiting:
-                half, q, i = steps[step]
-                sum_by_tensor(products, k_rows[:, :, i, :])
-                if step >= len(steps) - CHUNK_HEADS:
-                    store_keys(half, q, i - 1, 2, k_rows)
-                elif i == CHUNK_HEADS - 1:
-                    store_keys(half, q, 0, CHUNK_HEADS, k_rows)
-            waiting.clear()
+        waiting = []
+        keys = {}
+        turned_keys = {}
 
-        for step, (half, q, i) in enumerate(steps):
+        def rope(head, k_rows):
+            half, q, i = heads[head]
+            if summed_by_tensor(head):
+                products = turned_products(half, q * CHUNK_HEADS + i, keys[head])
+                waiting.append((head, products, k_rows))
+            else:
+                rope_by_gpsimd(half, turned_keys[head], k_rows[:, :, i, :])
+
+        for head in range(2):
+            keys[head] = project_keys(head)
+        finish()
+        for step in range(len(heads) // 2):
+            first, second = 2 * step, 2 * step + 1
+            half, q, i = heads[first]
             j = half * TILES + i
+            coming = [head for head in (first + 2, second + 2) if head < len(heads)]
+            unsummed, waiting = waiting, []
             if i == 0:
                 k_rows = results.tile([P, TILES, CHUNK_HEADS, HEAD_DIM], F32, tag="k_rows")
-            if i % 2 == 0:
-                v_rows = results.tile([P, 2, BANK], F32, tag="v_rows", bufs=4)
-            finish_keys()
-            finish_values(step, v_bank, v_rows[:, i % 2, :])
-            if summed_by_tensor(i):
-                products = turned_products(half, q * CHUNK_HEADS + i, keys)
-                waiting.append((step, products, k_rows))
-            else:
-                rope_by_gpsimd(half, turn_back(keys), k_rows[:, :, i, :])
-            if step in stage_1:
-                compress(*stage_1[step])
-            if step + 1 < len(steps):
-                keys = project_keys(step + 1)
-                v_bank = project_values(step + 1)
+            v_rows = results.tile([P, 2, BANK], F32, tag="v_rows", bufs=4)
+            for head in (first, second):
+                if summed_by_tensor(head):
+                    keys[head] = project_keys(head)
+                else:
+                    turned_keys[head] = turn_back(keys[head])
+            rope(first, k_rows)
             if step in grouping:
                 group_c(grouping[step])
+            finish()
+            rope(second, k_rows)
             if step in quantising:
                 quantise_c(quantising[step])
-            if step in pieces:
-                prepare(pieces[step], scalar_only)
-            else:
-                finish()
-            if i % 2 == 1:
-                nc.sync.dma_start(
-                    out=v_out[:, j - 1 : j + 1, q * BANK : (q + 1) * BANK], in_=v_rows[:]
-                )
-        finish_keys()
+            for head in coming:
+                if not summed_by_tensor(head):
+                    keys[head] = project_keys(head)
+            v_second = project_values(second)
+            finish_values(second, v_second, v_rows[:, 1, :])
+            v_first = project_values(first)
+            finish_values(first, v_first, v_rows[:, 0, :])
+            for piece in pieces.get(step, ()):
+                prepare(piece, scalar_only)
+            for part in stage_1.get(step, ()):
+                compress(*part)
+            if step in tables_to_turn:
+                turn_tables(*tables_to_turn[step])
+            for head, products, rows in unsummed:
+                sum_by_tensor(products, rows[:, :, heads[head][2], :])
+            if not coming:
+                store_keys(half, q, 0, 2, k_rows)
+            if i == 0 and unsummed:
+                last_half, last_q, _ = heads[first - 1]
+                store_keys(last_half, last_q, 0, CHUNK_HEADS, unsummed[-1][2])
+            nc.sync.dma_start(
+                out=v_out[:, j : j + 2, q * BANK : (q + 1) * BANK], in_=v_rows[:]
+            )
+            if i != 0 and not summed_by_tensor(second):
+                store_keys(half, q, 0, CHUNK_HEADS, k_rows)
+        for head, products, rows in waiting:
+            sum_by_tensor(products, rows[:, :, heads[head][2], :])
+        half, q, i = heads[-1]
+        store_keys(half, q, 2, 2, k_rows)

@@ -123,21 +123,21 @@ def tile_selfattention_pa_kernel(
 
         bkv = keep.tile([P, PACK], F32)
         bk = keep.tile([P, HEADS], F32)
-        tables_turned = keep.tile([P, 2, S], BF16)
+        tables_turned = keep.tile([P, 2, BANK], BF16)
 
         def spread_key_bias():
             bank = banks.tile([P, P], BF16, tag="vector")
             nc.tensor.transpose(bank[:], bk_rows[:], identity_bf16[:])
             nc.vector.tensor_copy(out=bk[:], in_=bank[:, :HEADS])
 
-        def turn_tables(plane, half):
+        def turn_tables(plane):
             bank = banks.tile([P, TILES, P], BF16, tag="scalar")
             for jj in range(TILES):
                 nc.tensor.transpose(
-                    bank[:, jj, :], tables[:, plane, half * TILES + jj, :], identity_bf16[:]
+                    bank[:, jj, :], tables[:, plane, TILES + jj, :], identity_bf16[:]
                 )
             nc.scalar.activation(
-                out=tables_turned[:, plane, half * BANK : (half + 1) * BANK],
+                out=tables_turned[:, plane, :],
                 in_=bank[:].rearrange("p j row -> p (j row)"),
                 func=IDENTITY,
                 scale=1.0 if plane == 0 else sign[:, :1],
@@ -262,7 +262,7 @@ def tile_selfattention_pa_kernel(
 
         def summed_by_tensor(head):
             half, q, i = heads[head]
-            return half == 1 and i != 0
+            return half == 1
 
         def through_scalar(head):
             half, q, i = heads[head]
@@ -323,34 +323,35 @@ def tile_selfattention_pa_kernel(
                 nc.tensor.transpose(bank[:, jj, :], kT[:, jj * P : (jj + 1) * P], identity[:])
             return bank
 
-        def rope_by_gpsimd(half, bank, rows):
-            products = results.tile([P, 2, TILES, HEAD_DIM], F32, tag="products")
+        def rope_products(half, bank, products):
             nc.vector.tensor_tensor(
-                out=products[:],
+                out=products,
                 in0=bank[:].unsqueeze(1).to_broadcast([P, 2, TILES, HEAD_DIM]),
                 in1=tables[:, :, half * TILES : (half + 1) * TILES, :],
                 op=MULT,
             )
+
+        def rope_sums(products, rows):
             nc.gpsimd.tensor_tensor(
-                out=rows[:, :, :HALF_DIM],
-                in0=products[:, 0, :, :HALF_DIM],
-                in1=products[:, 1, :, HALF_DIM:],
+                out=rows[:, :, :, :HALF_DIM],
+                in0=products[:, 0, :, :, :HALF_DIM],
+                in1=products[:, 1, :, :, HALF_DIM:],
                 op=SUBTRACT,
             )
             nc.gpsimd.tensor_tensor(
-                out=rows[:, :, HALF_DIM:],
-                in0=products[:, 0, :, HALF_DIM:],
-                in1=products[:, 1, :, :HALF_DIM],
+                out=rows[:, :, :, HALF_DIM:],
+                in0=products[:, 0, :, :, HALF_DIM:],
+                in1=products[:, 1, :, :, :HALF_DIM],
                 op=ADD,
             )
 
-        def turned_products(half, h, k_bank):
+        def turned_products(h, k_bank):
             products = results.tile([P, 2, BANK], F32, tag="turned_products")
             nc.vector.scalar_tensor_tensor(
                 out=products[:],
                 in0=k_bank[:].unsqueeze(1).to_broadcast([P, 2, BANK]),
                 scalar=bk[:, h : h + 1],
-                in1=tables_turned[:, :, half * BANK : (half + 1) * BANK],
+                in1=tables_turned[:],
                 op0=ADD,
                 op1=MULT,
             )
@@ -378,31 +379,28 @@ def tile_selfattention_pa_kernel(
         prepare(piece_x(0, 0), scalar_only)
         prepare(piece_x(0, 1), shared)
         prepare(piece_x(1, 0), scalar_only)
-        finish()
         spread_key_bias()
+        prepare(piece_x(1, 1), shared)
         compress(0, 0)
         compress(0, 1)
-        prepare(piece_x(1, 1), shared)
         finish()
-        prepare(piece_wk(0), shared)
-        group_c(0)
-        finish()
-        quantise_c(0)
         compress(1, 0)
         compress(1, 1)
+        for pair in range(2):
+            group_c(pair)
+            quantise_c(pair)
+        prepare(piece_wk(0), shared)
         prepare(piece_wv(0), scalar_only)
-        group_c(1)
-        quantise_c(1)
 
         pieces = {
             0: (piece_wk(1), piece_wv(1)), 1: (piece_wk(2), piece_x(2, 0)),
             2: (piece_x(2, 1), piece_wv(2)), 3: (piece_wk(3), piece_x(3, 0)),
             4: (piece_x(3, 1), piece_wv(3)),
         }
-        stage_1 = {3: ((2, 0),), 4: ((2, 1),), 5: ((3, 0), (3, 1))}
-        grouping = {5: 2, 6: 3}
-        quantising = {5: 2, 6: 3}
-        tables_to_turn = {6: (0, 1), 7: (1, 1)}
+        stage_1 = {4: ((2, 0),), 5: ((2, 1), (3, 0)), 6: ((3, 1),)}
+        grouping = {6: 2, 7: 3}
+        quantising = {6: 2, 7: 3}
+        tables_to_turn = {6: 0, 7: 1}
 
         k_out = out_0.rearrange("(p j) h d -> p j (h d)", j=S_TILES)
         v_out = out_1.rearrange("(p j) h d -> p j (h d)", j=S_TILES)
@@ -420,13 +418,13 @@ def tile_selfattention_pa_kernel(
         keys = {}
         turned_keys = {}
 
-        def rope(head, k_rows):
+        def rope(head, k_rows, products):
             half, q, i = heads[head]
             if summed_by_tensor(head):
-                products = turned_products(half, q * CHUNK_HEADS + i, keys[head])
-                waiting.append((head, products, k_rows))
+                turned = turned_products(q * CHUNK_HEADS + i, keys[head])
+                waiting.append((head, turned, k_rows))
             else:
-                rope_by_gpsimd(half, turned_keys[head], k_rows[:, :, i, :])
+                rope_products(half, turned_keys[head], products[:, :, :, head % 2, :])
 
         for head in range(2):
             keys[head] = project_keys(head)
@@ -445,13 +443,22 @@ def tile_selfattention_pa_kernel(
                     keys[head] = project_keys(head)
                 else:
                     turned_keys[head] = turn_back(keys[head])
-            rope(first, k_rows)
+            by_gpsimd = [head for head in (first, second) if not summed_by_tensor(head)]
+            products = None
+            if by_gpsimd:
+                products = results.tile([P, 2, TILES, 2, HEAD_DIM], F32, tag="products")
             if step in grouping:
                 group_c(grouping[step])
-            finish()
-            rope(second, k_rows)
+            rope(first, k_rows, products)
             if step in quantising:
                 quantise_c(quantising[step])
+            finish()
+            rope(second, k_rows, products)
+            if by_gpsimd:
+                these = slice(by_gpsimd[0] - first, by_gpsimd[-1] - first + 1)
+                rope_sums(
+                    products[:, :, :, these, :], k_rows[:, :, i + these.start : i + these.stop, :]
+                )
             for head in coming:
                 if not summed_by_tensor(head):
                     keys[head] = project_keys(head)
@@ -459,12 +466,12 @@ def tile_selfattention_pa_kernel(
             finish_values(second, v_second, v_rows[:, 1, :])
             v_first = project_values(first)
             finish_values(first, v_first, v_rows[:, 0, :])
-            for piece in pieces.get(step, ()):
-                prepare(piece, scalar_only)
             for part in stage_1.get(step, ()):
                 compress(*part)
+            for piece in pieces.get(step, ()):
+                prepare(piece, scalar_only)
             if step in tables_to_turn:
-                turn_tables(*tables_to_turn[step])
+                turn_tables(tables_to_turn[step])
             for head, products, rows in unsummed:
                 sum_by_tensor(products, rows[:, :, heads[head][2], :])
             if not coming:
@@ -478,6 +485,6 @@ def tile_selfattention_pa_kernel(
             if i != 0 and not summed_by_tensor(second):
                 store_keys(half, q, 0, CHUNK_HEADS, k_rows)
         for head, products, rows in waiting:
-            sum_by_tensor(products, rows[:, :, heads[head][2], :])
-        half, q, i = heads[-1]
-        store_keys(half, q, 2, 2, k_rows)
+            half, q, i = heads[head]
+            sum_by_tensor(products, rows[:, :, i, :])
+            store_keys(half, q, i, 1, rows)

@@ -143,6 +143,13 @@ def tile_selfattention_pa_kernel(
                 scale=1.0 if plane == 0 else sign[:, :1],
             )
 
+        def keep_clock(count):
+            zeros = stage.tile([P, BANK], BF16, tag="grouped", align_bytes=64)
+            nc.vector.memset(zeros[:], 0.0)
+            bank = banks.tile([P, BANK], F32, tag="vector")
+            for repeat in range(count):
+                nc.tensor.matmul(bank[:], zeros[:, :P], zeros[:], start=True, stop=True)
+
         def turn(row_passes, copies):
             grouped = stage.tile([P, BANK, PACK], BF16, tag="grouped", align_bytes=64)
             grouped_words = grouped[:].bitcast(F32)
@@ -373,6 +380,7 @@ def tile_selfattention_pa_kernel(
 
         scalar_only = (nc.scalar.copy, nc.scalar.copy)
         shared = (nc.scalar.copy, nc.vector.tensor_copy)
+        keep_clock(5)
         for t in range(PACK):
             prepare(piece_wkv(t), shared if t % 2 == 1 else scalar_only)
         nc.vector.tensor_copy(out=bkv[:], in_=bkv_bf16[:])
@@ -462,13 +470,15 @@ def tile_selfattention_pa_kernel(
             for head in coming:
                 if not summed_by_tensor(head):
                     keys[head] = project_keys(head)
+            for piece in pieces.get(step, ())[:1]:
+                prepare(piece, scalar_only)
             v_second = project_values(second)
             finish_values(second, v_second, v_rows[:, 1, :])
             v_first = project_values(first)
             finish_values(first, v_first, v_rows[:, 0, :])
             for part in stage_1.get(step, ()):
                 compress(*part)
-            for piece in pieces.get(step, ()):
+            for piece in pieces.get(step, ())[1:]:
                 prepare(piece, scalar_only)
             if step in tables_to_turn:
                 turn_tables(tables_to_turn[step])

@@ -40,7 +40,7 @@ def tile_selfattention_pa_kernel(
     nc = tc.nc
     with ExitStack() as pools:
         keep = pools.enter_context(tc.tile_pool(name="keep", bufs=1))
-        raw = pools.enter_context(tc.tile_pool(name="raw", bufs=16))
+        raw = pools.enter_context(tc.tile_pool(name="raw", bufs=12))
         stage = pools.enter_context(tc.tile_pool(name="stage", bufs=3))
         results = pools.enter_context(tc.tile_pool(name="results", bufs=3))
         banks = pools.enter_context(tc.psum_pool(name="banks", bufs=4))
@@ -123,21 +123,21 @@ def tile_selfattention_pa_kernel(
 
         bkv = keep.tile([P, PACK], F32)
         bk = keep.tile([P, HEADS], F32)
-        tables_turned = keep.tile([P, 2, BANK], BF16)
+        tables_turned = keep.tile([P, 2, S], BF16)
 
         def spread_key_bias():
             bank = banks.tile([P, P], BF16, tag="vector")
             nc.tensor.transpose(bank[:], bk_rows[:], identity_bf16[:])
             nc.vector.tensor_copy(out=bk[:], in_=bank[:, :HEADS])
 
-        def turn_tables(plane):
+        def turn_tables(plane, half):
             bank = banks.tile([P, TILES, P], BF16, tag="scalar")
             for jj in range(TILES):
                 nc.tensor.transpose(
-                    bank[:, jj, :], tables[:, plane, TILES + jj, :], identity_bf16[:]
+                    bank[:, jj, :], tables[:, plane, half * TILES + jj, :], identity_bf16[:]
                 )
             nc.scalar.activation(
-                out=tables_turned[:, plane, :],
+                out=tables_turned[:, plane, half * BANK : (half + 1) * BANK],
                 in_=bank[:].rearrange("p j row -> p (j row)"),
                 func=IDENTITY,
                 scale=1.0 if plane == 0 else sign[:, :1],
@@ -269,11 +269,11 @@ def tile_selfattention_pa_kernel(
 
         def summed_by_tensor(head):
             half, q, i = heads[head]
-            return half == 1
+            return (half == 1 and True) or (half == 0 and i >= 2)
 
         def through_scalar(head):
             half, q, i = heads[head]
-            return i % 2 == 1 or (half == 1 and i != 0 and head != len(heads) - 2)
+            return (half == 0 and i == 3) or (half == 1 and (True) and head != len(heads) - 2)
 
         def project_keys(head):
             half, q, i = heads[head]
@@ -298,9 +298,16 @@ def tile_selfattention_pa_kernel(
             )
             return kT
 
-        def project_values(head):
+        def place_of_values(head):
             half, q, i = heads[head]
-            j = half * TILES + i
+            if half == 0:
+                return i, q
+            q2, i2 = divmod(q * CHUNK_HEADS + i, 2 * TILES)
+            j2, part = divmod(i2, 2)
+            return TILES + j2, 2 * q2 + part
+
+        def project_values(head):
+            j, q = place_of_values(head)
             pos = slice(j * P, (j + 1) * P)
             cols = slice(q * BANK, (q + 1) * BANK)
             v_bank = banks.tile([P, BANK], F32, tag="scalar" if through_scalar(head) else "vector")
@@ -316,7 +323,7 @@ def tile_selfattention_pa_kernel(
             return v_bank
 
         def finish_values(head, v_bank, v_rows):
-            half, q, i = heads[head]
+            j, q = place_of_values(head)
             bias = bv_all[:, q * BANK : (q + 1) * BANK]
             if through_scalar(head):
                 nc.scalar.copy(out=v_rows, in_=v_bank[:])
@@ -352,13 +359,13 @@ def tile_selfattention_pa_kernel(
                 op=ADD,
             )
 
-        def turned_products(h, k_bank):
+        def turned_products(half, h, k_bank):
             products = results.tile([P, 2, BANK], F32, tag="turned_products")
             nc.vector.scalar_tensor_tensor(
                 out=products[:],
                 in0=k_bank[:].unsqueeze(1).to_broadcast([P, 2, BANK]),
                 scalar=bk[:, h : h + 1],
-                in1=tables_turned[:],
+                in1=tables_turned[:, :, half * BANK : (half + 1) * BANK],
                 op0=ADD,
                 op1=MULT,
             )
@@ -399,16 +406,16 @@ def tile_selfattention_pa_kernel(
             quantise_c(pair)
         prepare(piece_wk(0), shared)
         prepare(piece_wv(0), scalar_only)
+        prepare(piece_wk(1), scalar_only)
 
         pieces = {
-            0: (piece_wk(1), piece_wv(1)), 1: (piece_wk(2), piece_x(2, 0)),
-            2: (piece_x(2, 1), piece_wv(2)), 3: (piece_wk(3), piece_x(3, 0)),
-            4: (piece_x(3, 1), piece_wv(3)),
+            0: (piece_wv(1), piece_x(2, 0)), 1: (piece_wk(2), piece_x(2, 1)),
+            2: (piece_wv(2), piece_x(3, 0)), 3: (piece_wk(3), piece_x(3, 1)), 4: (piece_wv(3),),
         }
         stage_1 = {4: ((2, 0),), 5: ((2, 1), (3, 0)), 6: ((3, 1),)}
         grouping = {6: 2, 7: 3}
         quantising = {6: 2, 7: 3}
-        tables_to_turn = {6: 0, 7: 1}
+        tables_to_turn = {0: ((0, 0), (1, 0)), 6: ((0, 1),), 7: ((1, 1),)}
 
         k_out = out_0.rearrange("(p j) h d -> p j (h d)", j=S_TILES)
         v_out = out_1.rearrange("(p j) h d -> p j (h d)", j=S_TILES)
@@ -429,7 +436,7 @@ def tile_selfattention_pa_kernel(
         def rope(head, k_rows, products):
             half, q, i = heads[head]
             if summed_by_tensor(head):
-                turned = turned_products(q * CHUNK_HEADS + i, keys[head])
+                turned = turned_products(half, q * CHUNK_HEADS + i, keys[head])
                 waiting.append((head, turned, k_rows))
             else:
                 rope_products(half, turned_keys[head], products[:, :, :, head % 2, :])
@@ -440,7 +447,6 @@ def tile_selfattention_pa_kernel(
         for step in range(len(heads) // 2):
             first, second = 2 * step, 2 * step + 1
             half, q, i = heads[first]
-            j = half * TILES + i
             coming = [head for head in (first + 2, second + 2) if head < len(heads)]
             unsummed, waiting = waiting, []
             if i == 0:
@@ -480,20 +486,28 @@ def tile_selfattention_pa_kernel(
                 compress(*part)
             for piece in pieces.get(step, ())[1:]:
                 prepare(piece, scalar_only)
-            if step in tables_to_turn:
-                turn_tables(tables_to_turn[step])
+            for plane_and_half in tables_to_turn.get(step, ()):
+                turn_tables(*plane_and_half)
             for head, products, rows in unsummed:
                 sum_by_tensor(products, rows[:, :, heads[head][2], :])
-            if not coming:
-                store_keys(half, q, 0, 2, k_rows)
-            if i == 0 and unsummed:
-                last_half, last_q, _ = heads[first - 1]
-                store_keys(last_half, last_q, 0, CHUNK_HEADS, unsummed[-1][2])
-            nc.sync.dma_start(
-                out=v_out[:, j : j + 2, q * BANK : (q + 1) * BANK], in_=v_rows[:]
-            )
-            if i != 0 and not summed_by_tensor(second):
+            if unsummed:
+                last_half, last_q, last_i = heads[first - 2]
+                if last_half == 1:
+                    store_keys(last_half, last_q, last_i, 2, unsummed[0][2])
+                elif last_i != 0:
+                    store_keys(last_half, last_q, 0, CHUNK_HEADS, unsummed[0][2])
+            if half == 0 and i != 0 and not summed_by_tensor(second):
                 store_keys(half, q, 0, CHUNK_HEADS, k_rows)
+            j, v_chunk = place_of_values(first)
+            if half == 0:
+                nc.sync.dma_start(
+                    out=v_out[:, j : j + 2, v_chunk * BANK : (v_chunk + 1) * BANK], in_=v_rows[:]
+                )
+            else:
+                nc.sync.dma_start(
+                    out=v_out[:, j, v_chunk * BANK : (v_chunk + 2) * BANK],
+                    in_=v_rows[:].rearrange("p r c -> p (r c)"),
+                )
         for head, products, rows in waiting:
             half, q, i = heads[head]
             sum_by_tensor(products, rows[:, :, i, :])

from contextlib import ExitStack

import concourse.mybir as mybir
from concourse.masks import make_identity

F32 = mybir.dt.float32
BF16 = mybir.dt.bfloat16
U32 = mybir.dt.uint32
U8 = mybir.dt.uint8
FP8X4 = mybir.dt.float8_e4m3fn_x4
ADD = mybir.AluOpType.add
SUBTRACT = mybir.AluOpType.subtract
MULT = mybir.AluOpType.mult
IDENTITY = mybir.ActivationFunctionType.Identity

P = 128
PACK = 4
K_PASS = P * PACK
WORDS = K_PASS // 2
BANK = 512

S, D, CKV, HEADS, HEAD_DIM = 1024, 2048, 512, 16, 128
E = HEADS * HEAD_DIM
HALF_DIM = HEAD_DIM // 2
S_TILES = S // P
S_HALVES = S // BANK
TILES = BANK // P
PAIR = 2 * P
PAIRS = S // PAIR
D_PASSES = D // K_PASS
CHUNKS = E // BANK
CHUNK_HEADS = BANK // HEAD_DIM

FLOPS = 2 * S * D * CKV + 2 * 2 * S * CKV * E


def tile_selfattention_pa_kernel(
    tc, x, rope_cos, rope_sin, wkv_down, bkv_down, wk_up, bk_up, wv_up, bv_up, out_0, out_1
):
    nc = tc.nc
    with ExitStack() as pools:
        keep = pools.enter_context(tc.tile_pool(name="keep", bufs=1))
        raw = pools.enter_context(tc.tile_pool(name="raw", bufs=12))
        stage = pools.enter_context(tc.tile_pool(name="stage", bufs=3))
        results = pools.enter_context(tc.tile_pool(name="results", bufs=3))
        banks = pools.enter_context(tc.psum_pool(name="banks", bufs=4))
        pools.enter_context(tc.manual_schedule())

        identity = keep.tile([P, P], F32)
        make_identity(nc, identity[:])
        identity_bf16 = keep.tile([P, P], BF16)
        nc.gpsimd.tensor_copy(out=identity_bf16[:], in_=identity[:])
        exchange = keep.tile([P, P], F32)
        nc.gpsimd.tensor_copy(out=exchange[:, :HALF_DIM], in_=identity[:, HALF_DIM:])
        nc.gpsimd.tensor_copy(out=exchange[:, HALF_DIM:], in_=identity[:, :HALF_DIM])
        sign = keep.tile([P, 1], F32)
        nc.gpsimd.memset(sign[:], 1.0)
        nc.gpsimd.memset(sign[HALF_DIM:], -1.0)
        bk_rows = keep.tile([P, HEAD_DIM], BF16)
        nc.vector.memset(bk_rows[:], 0.0)

        def load_piece(shape, source):
            piece = raw.tile([P] + shape, BF16, tag="piece", name="piece")
            nc.sync.dma_start(out=piece[:], in_=source)
            return piece

        wkv_rows = wkv_down.rearrange("(p t) d -> p t d", t=PACK)
        x_rows = x.rearrange("(p j) d -> p j d", j=S_TILES)
        wk_rows = wk_up.rearrange("(h p) c -> p h c", p=P)
        wv_rows = wv_up.rearrange("(h p) c -> p h c", p=P)

        wkv_pieces = [load_piece([D], wkv_rows[:, t, :]) for t in range(PACK)]
        bkv_bf16 = keep.tile([P, PACK], BF16)
        nc.sync.dma_start(out=bkv_bf16[:], in_=bkv_down.rearrange("(p t) -> p t", t=PACK))
        nc.sync.dma_start(out=bk_rows[:HEADS, :], in_=bk_up.rearrange("(h d) -> h d", d=HEAD_DIM))

        x_pieces = {}
        wk_pieces = {}
        wv_pieces = {}
        bv_all = keep.tile([P, E], BF16)

        def load_x(pair):
            for g2 in range(2):
                x_pieces[pair, g2] = load_piece(
                    [2, D // 2], x_rows[:, 2 * pair : 2 * pair + 2, g2 * D // 2 : (g2 + 1) * D // 2]
                )

        def load_up_weights(q):
            heads = slice(q * CHUNK_HEADS, (q + 1) * CHUNK_HEADS)
            wk_pieces[q] = load_piece([CHUNK_HEADS, CKV], wk_rows[:, heads, :])
            wv_pieces[q] = load_piece([CHUNK_HEADS, CKV], wv_rows[:, heads, :])

        def load_value_bias(cols):
            nc.sync.dma_start(out=bv_all[:, cols], in_=bv_up[cols].partition_broadcast(P))

        load_x(0)
        load_x(1)
        load_up_weights(0)
        tables = keep.tile([P, 2, S_TILES, HEAD_DIM], BF16)
        sin_raw = keep.tile([P, S_TILES, HEAD_DIM], BF16)
        nc.sync.dma_start(out=tables[:, 0], in_=rope_cos.rearrange("(p j) d -> p j d", j=S_TILES))
        nc.sync.dma_start(out=sin_raw[:], in_=rope_sin.rearrange("(p j) d -> p j d", j=S_TILES))
        nc.gpsimd.tensor_copy(out=tables[:, 1, :, :HALF_DIM], in_=sin_raw[:, :, HALF_DIM:])
        nc.gpsimd.tensor_copy(out=tables[:, 1, :, HALF_DIM:], in_=sin_raw[:, :, :HALF_DIM])
        load_value_bias(slice(0, BANK))
        load_up_weights(1)
        load_value_bias(slice(BANK, E))
        load_up_weights(2)
        load_x(2)
        load_up_weights(3)
        load_x(3)

        wkv_codes = keep.tile([P, PACK, D_PASSES, P], U32, align_bytes=64)
        wkv_scales = keep.tile([P, PACK, D_PASSES, P], U8, align_bytes=64)
        x_codes = keep.tile([P, PAIRS, D_PASSES, PAIR], U32, align_bytes=64)
        x_scales = keep.tile([P, PAIRS, D_PASSES, PAIR], U8, align_bytes=64)
        c_codes = keep.tile([P, S], U32, align_bytes=64)
        c_scales = keep.tile([P, S], U8, align_bytes=64)
        wk_codes = keep.tile([P, E], U32, align_bytes=64)
        wk_scales = keep.tile([P, E], U8, align_bytes=64)
        wv_codes = keep.tile([P, E], U32, align_bytes=64)
        wv_scales = keep.tile([P, E], U8, align_bytes=64)

        bkv = keep.tile([P, PACK], F32)
        bk = keep.tile([P, HEADS], F32)
        tables_turned = keep.tile([P, 2, S], BF16)

        def spread_key_bias():
            bank = banks.tile([P, P], BF16, tag="vector")
            nc.tensor.transpose(bank[:], bk_rows[:], identity_bf16[:])
            nc.vector.tensor_copy(out=bk[:], in_=bank[:, :HEADS])

        def turn_tables(plane, half):
            bank = banks.tile([P, TILES, P], BF16, tag="scalar")
            for jj in range(TILES):
                nc.tensor.transpose(
                    bank[:, jj, :], tables[:, plane, half * TILES + jj, :], identity_bf16[:]
                )
            nc.scalar.activation(
                out=tables_turned[:, plane, half * BANK : (half + 1) * BANK],
                in_=bank[:].rearrange("p j row -> p (j row)"),
                func=IDENTITY,
                scale=1.0 if plane == 0 else sign[:, :1],
            )

        def keep_clock(count):
            zeros = stage.tile([P, BANK], BF16, tag="grouped", align_bytes=64)
            nc.vector.memset(zeros[:], 0.0)
            bank = banks.tile([P, BANK], F32, tag="vector")
            for repeat in range(count):
                nc.tensor.matmul(bank[:], zeros[:, :P], zeros[:], start=True, stop=True)

        def turn(row_passes, copies):
            grouped = stage.tile([P, BANK, PACK], BF16, tag="grouped", align_bytes=64)
            grouped_words = grouped[:].bitcast(F32)
            for b in range(2):
                reader = "scalar" if copies[b] == nc.scalar.copy else "vector"
                bank = banks.tile([P, 2, 2, P], F32, tag=reader)
                for r in range(2):
                    for u in range(2):
                        nc.tensor.transpose(
                            bank[:, r, u, :], row_passes[2 * b + r][:, u:WORDS:2], identity[:]
                        )
                copies[b](
                    out=grouped_words[:, b * PAIR : (b + 1) * PAIR, :].rearrange(
                        "p (r row) u -> p r row u", r=2
                    ),
                    in_=bank[:].rearrange("p r u row -> p r row u"),
                )
            return grouped

        def quantise(grouped, codes, scales):
            nc.vector.quantize_mx(
                out=codes.bitcast(FP8X4), scales=scales,
                in_=grouped[:].rearrange("p row t -> p (row t)"),
            )

        def piece_wkv(t):
            words = wkv_pieces[t][:].bitcast(F32)
            passes = [words[:, g * WORDS : (g + 1) * WORDS] for g in range(D_PASSES)]
            return (
                passes,
                wkv_codes[:, t].rearrange("p g row -> p (g row)"),
                wkv_scales[:, t].rearrange("p g row -> p (g row)"),
            )

        def piece_x(pair, g2):
            words = x_pieces[pair, g2][:].bitcast(F32)
            passes = [words[:, r, g * WORDS : (g + 1) * WORDS] for g in range(2) for r in range(2)]
            gs = slice(2 * g2, 2 * g2 + 2)
            return (
                passes,
                x_codes[:, pair, gs, :].rearrange("p g row -> p (g row)"),
                x_scales[:, pair, gs, :].rearrange("p g row -> p (g row)"),
            )

        def piece_up(pieces, codes, scales, q):
            words = pieces[q][:].bitcast(F32)
            cols = slice(q * BANK, (q + 1) * BANK)
            return [words[:, i, :] for i in range(CHUNK_HEADS)], codes[:, cols], scales[:, cols]

        def piece_wk(q):
            return piece_up(wk_pieces, wk_codes, wk_scales, q)

        def piece_wv(q):
            return piece_up(wv_pieces, wv_codes, wv_scales, q)

        unfinished = []

        def finish():
            for grouped, codes, scales in unfinished:
                quantise(grouped, codes, scales)
            unfinished.clear()

        def prepare(piece, copies):
            row_passes, codes, scales = piece
            grouped = turn(row_passes, copies)
            finish()
            unfinished.append((grouped, codes, scales))

        c_rows = {}
        c_grouped = {}

        def compress(pair, t2):
            if t2 == 0:
                c_rows[pair] = stage.tile([P, PACK, PAIR], BF16, tag="c_rows", name="c_rows")
            c_bank = banks.tile([P, 2, PAIR], F32, tag="scalar")
            for i in range(2):
                t = 2 * t2 + i
                for g in range(D_PASSES):
                    nc.tensor.matmul_mx(
                        out=c_bank[:, i, :],
                        lhsT=wkv_codes[:, t, g, :].bitcast(FP8X4),
                        lhsT_scale=wkv_scales[:, t, g, :],
                        rhs=x_codes[:, pair, g, :].bitcast(FP8X4),
                        rhs_scale=x_scales[:, pair, g, :],
                        start=(g == 0),
                        stop=(g == D_PASSES - 1),
                    )
            for i in range(2):
                t = 2 * t2 + i
                nc.scalar.activation(
                    out=c_rows[pair][:, t, :], in_=c_bank[:, i, :], func=IDENTITY,
                    bias=bkv[:, t : t + 1], scale=1.0,
                )

        def group_c(pair):
            c_grouped[pair] = stage.tile(
                [P, PAIR, PACK], BF16, tag="c_grouped", name="c_grouped", align_bytes=64
            )
            nc.vector.tensor_copy(
                out=c_grouped[pair][:], in_=c_rows[pair][:].rearrange("p t s -> p s t")
            )

        def quantise_c(pair):
            pos = slice(pair * PAIR, (pair + 1) * PAIR)
            nc.vector.quantize_mx(
                out=c_codes[:, pos].bitcast(FP8X4),
                scales=c_scales[:, pos],
                in_=c_grouped[pair][:].rearrange("p s t -> p (s t)"),
            )

        heads = [
            (half, q, i)
            for half in range(S_HALVES)
            for q in range(CHUNKS)
            for i in range(CHUNK_HEADS)
        ]

        def summed_by_tensor(head):
            half, q, i = heads[head]
            return (half == 1 and True) or (half == 0 and i >= 2)

        def through_scalar(head):
            half, q, i = heads[head]
            return (half == 0 and i == 3) or (half == 1 and (True) and head != len(heads) - 2)

        def project_keys(head):
            half, q, i = heads[head]
            h = q * CHUNK_HEADS + i
            pos = slice(half * BANK, (half + 1) * BANK)
            cols = slice(h * HEAD_DIM, (h + 1) * HEAD_DIM)
            k_bank = banks.tile([P, BANK], F32, tag="vector" if summed_by_tensor(head) else "scalar")
            nc.tensor.matmul_mx(
                out=k_bank[:],
                lhsT=wk_codes[:, cols].bitcast(FP8X4),
                lhsT_scale=wk_scales[:, cols],
                rhs=c_codes[:, pos].bitcast(FP8X4),
                rhs_scale=c_scales[:, pos],
                start=True,
                stop=True,
            )
            if summed_by_tensor(head):
                return k_bank
            kT = stage.tile([P, BANK], F32, tag="kT")
            nc.scalar.activation(
                out=kT[:], in_=k_bank[:], func=IDENTITY, bias=bk[:, h : h + 1], scale=1.0
            )
            return kT

        def place_of_values(head):
            half, q, i = heads[head]
            if half == 0:
                return i, q
            q2, i2 = divmod(q * CHUNK_HEADS + i, 2 * TILES)
            j2, part = divmod(i2, 2)
            return TILES + j2, 2 * q2 + part

        def project_values(head):
            j, q = place_of_values(head)
            pos = slice(j * P, (j + 1) * P)
            cols = slice(q * BANK, (q + 1) * BANK)
            v_bank = banks.tile([P, BANK], F32, tag="scalar" if through_scalar(head) else "vector")
            nc.tensor.matmul_mx(
                out=v_bank[:],
                lhsT=c_codes[:, pos].bitcast(FP8X4),
                lhsT_scale=c_scales[:, pos],
                rhs=wv_codes[:, cols].bitcast(FP8X4),
                rhs_scale=wv_scales[:, cols],
                start=True,
                stop=True,
            )
            return v_bank

        def finish_values(head, v_bank, v_rows):
            j, q = place_of_values(head)
            bias = bv_all[:, q * BANK : (q + 1) * BANK]
            if through_scalar(head):
                nc.scalar.copy(out=v_rows, in_=v_bank[:])
                nc.gpsimd.tensor_tensor(out=v_rows, in0=v_rows, in1=bias, op=ADD)
            else:
                nc.vector.tensor_tensor(out=v_rows, in0=v_bank[:], in1=bias, op=ADD)

        def turn_back(kT):
            bank = banks.tile([P, TILES, HEAD_DIM], F32, tag="vector")
            for jj in range(TILES):
                nc.tensor.transpose(bank[:, jj, :], kT[:, jj * P : (jj + 1) * P], identity[:])
            return bank

        def rope_products(half, bank, products):
            nc.vector.tensor_tensor(
                out=products,
                in0=bank[:].unsqueeze(1).to_broadcast([P, 2, TILES, HEAD_DIM]),
                in1=tables[:, :, half * TILES : (half + 1) * TILES, :],
                op=MULT,
            )

        def rope_sums(products, rows):
            nc.gpsimd.tensor_tensor(
                out=rows[:, :, :, :HALF_DIM],
                in0=products[:, 0, :, :, :HALF_DIM],
                in1=products[:, 1, :, :, HALF_DIM:],
                op=SUBTRACT,
            )
            nc.gpsimd.tensor_tensor(
                out=rows[:, :, :, HALF_DIM:],
                in0=products[:, 0, :, :, HALF_DIM:],
                in1=products[:, 1, :, :, :HALF_DIM],
                op=ADD,
            )

        def turned_products(half, h, k_bank):
            products = results.tile([P, 2, BANK], F32, tag="turned_products")
            nc.vector.scalar_tensor_tensor(
                out=products[:],
                in0=k_bank[:].unsqueeze(1).to_broadcast([P, 2, BANK]),
                scalar=bk[:, h : h + 1],
                in1=tables_turned[:, :, half * BANK : (half + 1) * BANK],
                op0=ADD,
                op1=MULT,
            )
            return products

        def sum_by_tensor(products, rows):
            bank = banks.tile([P, TILES, HEAD_DIM], F32, tag="scalar")
            for jj in range(TILES):
                pos = slice(jj * P, (jj + 1) * P)
                nc.tensor.matmul(
                    bank[:, jj, :], products[:, 0, pos], identity[:],
                    start=True, stop=False, is_transpose=True,
                )
                nc.tensor.matmul(
                    bank[:, jj, :], products[:, 1, pos], exchange[:],
                    start=False, stop=True, is_transpose=True,
                )
            nc.scalar.copy(out=rows, in_=bank[:])

        scalar_only = (nc.scalar.copy, nc.scalar.copy)
        shared = (nc.scalar.copy, nc.vector.tensor_copy)
        keep_clock(5)
        for t in range(PACK):
            prepare(piece_wkv(t), shared if t % 2 == 1 else scalar_only)
        nc.vector.tensor_copy(out=bkv[:], in_=bkv_bf16[:])
        prepare(piece_x(0, 0), scalar_only)
        prepare(piece_x(0, 1), shared)
        prepare(piece_x(1, 0), scalar_only)
        spread_key_bias()
        prepare(piece_x(1, 1), shared)
        compress(0, 0)
        compress(0, 1)
        finish()
        compress(1, 0)
        compress(1, 1)
        for pair in range(2):
            group_c(pair)
            quantise_c(pair)
        prepare(piece_wk(0), shared)
        prepare(piece_wv(0), scalar_only)
        prepare(piece_wk(1), scalar_only)

        pieces = {
            0: (piece_wv(1), piece_x(2, 0)), 1: (piece_wk(2), piece_x(2, 1)),
            2: (piece_wv(2), piece_x(3, 0)), 3: (piece_wk(3), piece_x(3, 1)), 4: (piece_wv(3),),
        }
        stage_1 = {4: ((2, 0),), 5: ((2, 1), (3, 0)), 6: ((3, 1),)}
        grouping = {6: 2, 7: 3}
        quantising = {6: 2, 7: 3}
        tables_to_turn = {0: ((0, 0), (1, 0)), 6: ((0, 1),), 7: ((1, 1),)}

        k_out = out_0.rearrange("(p j) h d -> p j (h d)", j=S_TILES)
        v_out = out_1.rearrange("(p j) h d -> p j (h d)", j=S_TILES)

        def store_keys(half, q, first, count, k_rows):
            start = (q * CHUNK_HEADS + first) * HEAD_DIM
            nc.sync.dma_start(
                out=k_out[
                    :, half * TILES : (half + 1) * TILES, start : start + count * HEAD_DIM
                ],
                in_=k_rows[:, :, first : first + count, :].rearrange("p j h d -> p j (h d)"),
            )

        waiting = []
        keys = {}
        turned_keys = {}

        def rope(head, k_rows, products):
            half, q, i = heads[head]
            if summed_by_tensor(head):
                turned = turned_products(half, q * CHUNK_HEADS + i, keys[head])
                waiting.append((head, turned, k_rows))
            else:
                rope_products(half, turned_keys[head], products[:, :, :, head % 2, :])

        for head in range(2):
            keys[head] = project_keys(head)
        finish()
        for step in range(len(heads) // 2):
            first, second = 2 * step, 2 * step + 1
            half, q, i = heads[first]
            coming = [head for head in (first + 2, second + 2) if head < len(heads)]
            unsummed, waiting = waiting, []
            if i == 0:
                k_rows = results.tile([P, TILES, CHUNK_HEADS, HEAD_DIM], F32, tag="k_rows")
            v_rows = results.tile([P, 2, BANK], F32, tag="v_rows", bufs=4)
            for head in (first, second):
                if summed_by_tensor(head):
                    keys[head] = project_keys(head)
                else:
                    turned_keys[head] = turn_back(keys[head])
            by_gpsimd = [head for head in (first, second) if not summed_by_tensor(head)]
            products = None
            if by_gpsimd:
                products = results.tile([P, 2, TILES, 2, HEAD_DIM], F32, tag="products")
            if step in grouping:
                group_c(grouping[step])
            rope(first, k_rows, products)
            if step in quantising:
                quantise_c(quantising[step])
            finish()
            rope(second, k_rows, products)
            if by_gpsimd:
                these = slice(by_gpsimd[0] - first, by_gpsimd[-1] - first + 1)
                rope_sums(
                    products[:, :, :, these, :], k_rows[:, :, i + these.start : i + these.stop, :]
                )
            for head in coming:
                if not summed_by_tensor(head):
                    keys[head] = project_keys(head)
            for piece in pieces.get(step, ())[:1]:
                prepare(piece, scalar_only)
            v_second = project_values(second)
            finish_values(second, v_second, v_rows[:, 1, :])
            v_first = project_values(first)
            finish_values(first, v_first, v_rows[:, 0, :])
            for part in stage_1.get(step, ()):
                compress(*part)
            for piece in pieces.get(step, ())[1:]:
                prepare(piece, scalar_only)
            for plane_and_half in tables_to_turn.get(step, ()):
                turn_tables(*plane_and_half)
            for head, products, rows in unsummed:
                sum_by_tensor(products, rows[:, :, heads[head][2], :])
            if unsummed:
                last_half, last_q, last_i = heads[first - 2]
                if last_half == 1:
                    store_keys(last_half, last_q, last_i, 2, unsummed[0][2])
                elif last_i != 0:
                    store_keys(last_half, last_q, 0, CHUNK_HEADS, unsummed[0][2])
            if half == 0 and i != 0 and not summed_by_tensor(second):
                store_keys(half, q, 0, CHUNK_HEADS, k_rows)
            j, v_chunk = place_of_values(first)
            if half == 0:
                nc.sync.dma_start(
                    out=v_out[:, j : j + 2, v_chunk * BANK : (v_chunk + 1) * BANK], in_=v_rows[:]
                )
            else:
                nc.sync.dma_start(
                    out=v_out[:, j, v_chunk * BANK : (v_chunk + 2) * BANK],
                    in_=v_rows[:].rearrange("p r c -> p (r c)"),
                )
        for head, products, rows in waiting:
            half, q, i = heads[head]
            sum_by_tensor(products, rows[:, :, i, :])
            store_keys(half, q, i, 1, rows)
